import numpy as np
import ml_dtypes


def mxq(x, axis, fmt="e4m3"):
    dtype, down = {"e4m3": (ml_dtypes.float8_e4m3fn, 7), "e5m2": (ml_dtypes.float8_e5m2, 14)}[fmt]
    v = np.moveaxis(np.asarray(x, np.float32).astype(ml_dtypes.bfloat16).astype(np.float64), axis, -1)
    blocks = v.reshape(v.shape[:-1] + (-1, 32))
    amax = np.abs(blocks).max(-1, keepdims=True)
    byte = np.maximum(np.where(amax > 0, np.frexp(amax)[1] - 1 + 127, 0) - down, 1)
    scale = np.exp2(byte - 127.0)
    codes = (blocks / scale).astype(np.float32).astype(dtype).astype(np.float64)
    return np.moveaxis((codes * scale).reshape(v.shape), -1, axis)


WIDE = False


def mx_kscale(k):
    if not WIDE:
        return np.ones(k)
    levels = np.array([30, -30])
    if k % 512:
        return np.exp2(np.random.permutation(np.resize(levels, k // 32))).repeat(32)
    a = np.empty((k // 512, 16))
    for p in range(k // 512):
        a[p, :8] = np.random.permutation(np.resize(levels, 8))
        for g in range(8):
            far = levels[np.abs(levels - a[p, g]) >= 10]
            a[p, g + 8] = far[np.random.randint(len(far))]
    return np.exp2(a.ravel()).repeat(32)


BF16 = ml_dtypes.bfloat16


def bf(x):
    return np.asarray(x, np.float32).astype(BF16)


def f64(x):
    return np.asarray(x).astype(np.float64)


B, DIN, H1, H2, N, I, K, O = 1024, 2048, 1024, 512, 32, 16, 256, 16
NI = N * I
KO = K * O
SQ_EPS = 1e-8


def squash(t):
    sq = np.sum(t * t, axis=-1, keepdims=True)
    return (sq / (1.0 + sq)) * t / np.sqrt(sq + SQ_EPS)


def setup_inputs():
    s = mx_kscale(NI).reshape(N, I)
    return {"p": bf(np.random.standard_normal((B, N, I)) * s),
            "Wr": bf(np.random.standard_normal((N, K, O, I)) * K / np.sqrt(NI * O) / s[:, None, None, :])}


def reference(p, Wr):
    c = 1.0 / K
    pf = f64(p).reshape(B, NI)
    wf = f64(Wr).transpose(0, 3, 1, 2).reshape(NI, KO)
    s = (mxq(pf, 1, "e5m2") @ mxq(wf, 0, "e5m2")).reshape(B, K, O) * c
    return squash(s)

@@ -1,0 +1,309 @@
+from contextlib import ExitStack
+
+import concourse.mybir as mybir
+from concourse.masks import make_identity
+
+B, N, I, K, O = 1024, 32, 16, 256, 16
+FLOPS = 2 * B * N * I * K * O
+SQ_EPS = 1e-8
+
+F32 = mybir.dt.float32
+BF16 = mybir.dt.bfloat16
+U32 = mybir.dt.uint32
+U8 = mybir.dt.uint8
+FP8X4 = mybir.dt.float8_e5m2_x4
+ACT = mybir.ActivationFunctionType
+ALU = mybir.AluOpType
+
+P = 128
+QUADS = 4
+TILES = B // P
+HALVES = K // P
+STEPS = [(h, t) for h in range(HALVES) for t in range(TILES)]
+ROUTE = "DPPQPPQPPQPPQPPD"
+SUM_LAG = 7
+DIRECT_LAG = 5
+RED_LAG = 8
+ROOT_LAG = 1
+NORM_LAG = 2
+FAC_LAG = 3
+OUT_LAG = 15
+NORM_BANKS = [0, 1, 2]
+LATE_NORM_BANKS = [0, 1, 2, 6]
+OUT_BANKS = [3, 4, 5]
+PREP_BANKS = [3, 4, 5, 6]
+Q_BANK = 7
+PREP_START = 4
+PREP_EVERY = 2
+HEAD_ENG = "svsvsvsv"
+PREP_ENG = "vsvsvsvsvsv"
+TAIL_SPLIT = 2
+
+
+def tile_capsulenetwork_pb_kernel(tc, p, Wr, out):
+    nc = tc.nc
+    p2 = p.rearrange("(t b) n i -> b t (n i)", b=P)
+    out2 = out.rearrange("b j o -> b (j o)")
+
+    with ExitStack() as ctx:
+        keep = ctx.enter_context(tc.tile_pool(name="keep", bufs=1))
+        work = ctx.enter_context(tc.tile_pool(name="work", bufs=3))
+        psum = ctx.enter_context(tc.psum_pool(name="psum", bufs=1))
+        ctx.enter_context(tc.manual_schedule())
+
+        def bank(index, shape):
+            return psum.tile(shape, F32, name="bank%d" % index, tag="bank%d" % index)
+
+        p_raw = keep.tile([P, TILES, N * I], BF16, name="p_raw", align_bytes=64)
+        w_raw = {}
+
+        def load_w(h, o0, o1, n0, n1):
+            t = keep.tile([P, n1 - n0, (o1 - o0) * I], BF16, name="w_raw_%d_%d_%d" % (h, o0, n0), align_bytes=64)
+            nc.sync.dma_start(out=t[:], in_=Wr[n0:n1, h * P:(h + 1) * P, o0:o1, :].rearrange("n j o i -> j n (o i)"))
+            w_raw[(h, o0, n0)] = t
+
+        nc.sync.dma_start(out=p_raw[:, 0:2, :], in_=p2[:, 0:2, :])
+        load_w(0, 0, 8, 0, 16)
+        load_w(0, 0, 8, 16, 32)
+        load_w(0, 8, 16, 0, 16)
+        load_w(0, 8, 16, 16, 32)
+        nc.sync.dma_start(out=p_raw[:, 2:4, :], in_=p2[:, 2:4, :])
+        load_w(1, 0, 8, 0, 16)
+        load_w(1, 0, 8, 16, 32)
+        load_w(1, 8, 16, 0, 16)
+        load_w(1, 8, 16, 16, 32)
+        nc.sync.dma_start(out=p_raw[:, 4:TILES, :], in_=p2[:, 4:TILES, :])
+
+        ident = keep.tile([P, P], F32, name="ident")
+        make_identity(nc, ident[:])
+
+        w_sorted = [keep.tile([P, O, 2, N, 4], F32, name="w_sorted%d" % h, align_bytes=64) for h in range(HALVES)]
+        w_codes = [[keep.tile([P, 4 * P], U32, name="w_codes%d_%d" % (h, c), align_bytes=64) for c in range(QUADS)] for h in range(HALVES)]
+        w_scales = [[keep.tile([P, 4 * P], U8, name="w_scales%d_%d" % (h, c), align_bytes=64) for c in range(QUADS)] for h in range(HALVES)]
+        p_codes = [keep.tile([P, 2 * P], U32, name="p_codes%d" % g, align_bytes=64) for g in range(TILES // 2)]
+        p_scales = [keep.tile([P, 2 * P], U8, name="p_scales%d" % g, align_bytes=64) for g in range(TILES // 2)]
+
+        def sort_w(h, o0, o1, n0, n1):
+            src = w_raw[(h, o0, n0)][:].rearrange("p n x -> p (n x)").bitcast(F32)
+            nc.vector.tensor_copy(
+                out=w_sorted[h][:, o0:o1, :, n0:n1, :],
+                in_=src.rearrange("p (n o i u) -> p o u n i", n=n1 - n0, i=4, u=2),
+            )
+
+        turned = {}
+        grouped = {}
+
+        def turn_w(h, pair, bank_index):
+            t = bank(bank_index, [P, 2, 2, P])
+            for i in range(2):
+                for u in range(2):
+                    nc.tensor.transpose(
+                        t[:, i, u, :], w_sorted[h][:, 2 * pair + i, u, :, :].rearrange("p n i -> p (n i)"), ident[:]
+                    )
+            turned[("w", h, pair)] = t
+
+        def turn_p(g, bank_index):
+            t = bank(bank_index, [P, 2, 2, P])
+            for i in range(2):
+                words = p_raw[:, 2 * g + i, :].bitcast(F32)
+                for u in range(2):
+                    nc.tensor.transpose(t[:, i, u, :], words[:, u:2 * P:2], ident[:])
+            turned[("p", g)] = t
+
+        def copy_on(engine, dst, src):
+            if engine == "scalar":
+                nc.scalar.copy(out=dst, in_=src)
+            else:
+                nc.vector.tensor_copy(out=dst, in_=src)
+
+        def group_w(h, pair, engine):
+            if pair % 2 == 0:
+                grouped[("w", h, pair // 2)] = work.tile([P, 16 * P], BF16, name="w_grouped", align_bytes=64)
+            dst = grouped[("w", h, pair // 2)][:, (pair % 2) * 8 * P:(pair % 2 + 1) * 8 * P].bitcast(F32)
+            copy_on(engine, dst.rearrange("p (o j u) -> p o j u", o=2, u=2), turned[("w", h, pair)][:].rearrange("p o u j -> p o j u"))
+
+        def group_p(g, engine):
+            grouped[("p", g)] = work.tile([P, 8 * P], BF16, name="p_grouped", align_bytes=64)
+            dst = grouped[("p", g)][:].bitcast(F32)
+            copy_on(engine, dst.rearrange("p (t b u) -> p t b u", t=2, u=2), turned[("p", g)][:].rearrange("p t u b -> p t b u"))
+
+        def quantize_w(h, c):
+            nc.vector.quantize_mx(out=w_codes[h][c][:].bitcast(FP8X4), scales=w_scales[h][c][:], in_=grouped[("w", h, c)][:])
+
+        def quantize_p(g):
+            nc.vector.quantize_mx(out=p_codes[g][:].bitcast(FP8X4), scales=p_scales[g][:], in_=grouped[("p", g)][:])
+
+        slots = len(STEPS) * QUADS
+        norm_banks = {}
+        squares = {}
+        parts = {s: [] for s in range(len(STEPS))}
+        pair_tiles = {}
+        q_of = {}
+        small = {}
+        out_tiles = {}
+        prod_banks = {}
+
+        def p_operand(t):
+            cols = slice((t % 2) * P, (t % 2 + 1) * P)
+            return p_codes[t // 2][:, cols].bitcast(FP8X4), p_scales[t // 2][:, cols]
+
+        def product_by_rows(slot, bank_index):
+            s, c = divmod(slot, QUADS)
+            h, t = STEPS[s]
+            acc = bank(bank_index, [P, 4 * P])
+            codes, scales = p_operand(t)
+            nc.tensor.matmul_mx(out=acc[:], lhsT=codes, lhsT_scale=scales, rhs=w_codes[h][c][:].bitcast(FP8X4),
+                                rhs_scale=w_scales[h][c][:], start=True, stop=True)
+            return acc
+
+        def matmul_for_norm(slot):
+            s, c = divmod(slot, QUADS)
+            h, t = STEPS[s]
+            banks = NORM_BANKS if slot < OUT_LAG else LATE_NORM_BANKS
+            bank_index = banks[slot % len(banks)]
+            if ROUTE[s] == "Q":
+                norm_banks[slot] = product_by_rows(slot, bank_index)
+                return
+            acc = bank(bank_index, [P, 4 * P])
+            codes, scales = p_operand(t)
+            for i in range(4):
+                cols = slice(i * P, (i + 1) * P)
+                nc.tensor.matmul_mx(out=acc[:, cols], lhsT=w_codes[h][c][:, cols].bitcast(FP8X4), lhsT_scale=w_scales[h][c][:, cols],
+                                    rhs=codes, rhs_scale=scales, start=True, stop=True)
+            norm_banks[slot] = acc
+
+        def square_and_add(slot):
+            s, c = divmod(slot, QUADS)
+            sq = work.tile([P, 4 * P], F32, name="sq", bufs=8)
+            if ROUTE[s] == "Q":
+                nc.scalar.activation(out=sq[:].rearrange("p (j o) -> p j o", o=4), in_=norm_banks[slot][:].rearrange("p (o j) -> p j o", o=4),
+                                     func=ACT.Square, scale=1.0 / K)
+            else:
+                nc.scalar.activation(out=sq[:], in_=norm_banks[slot][:], func=ACT.Square, scale=1.0 / K)
+            squares[slot] = sq
+            if ROUTE[s] == "D":
+                parts[s].append(sq[:])
+            elif c % 2 == 1:
+                if c == 1:
+                    pair_tiles[s] = work.tile([P, 2, 4 * P], F32, name="pair_sum", bufs=4)
+                nc.gpsimd.tensor_tensor(out=pair_tiles[s][:, c // 2, :], in0=squares[slot - 1][:], in1=sq[:], op=ALU.add)
+                parts[s].append(pair_tiles[s][:, c // 2, :])
+
+        def sum_squares(s):
+            if ROUTE[s] == "Q":
+                q = work.tile([P, P], F32, name="q_sbuf")
+                nc.vector.tensor_reduce(out=q[:], in_=pair_tiles[s][:].rearrange("p a (j o) -> p j a o", o=4), axis=mybir.AxisListType.XY, op=ALU.add)
+            else:
+                q = bank(Q_BANK, [P, P])
+                blocks = [part[:, x * P:(x + 1) * P] for part in parts[s] for x in range(4)]
+                for n, block in enumerate(blocks):
+                    nc.tensor.matmul(out=q[:], lhsT=block, rhs=ident[:], is_transpose=True, start=(n == 0), stop=(n == len(blocks) - 1))
+            q_of[s] = q
+
+        def roots(s):
+            a = work.tile([P, P], F32, name="inv_norm")
+            g = work.tile([P, P], F32, name="inv_root")
+            u = work.tile([P, P], F32, name="inv_one_plus")
+            nc.scalar.activation(out=g[:], in_=q_of[s][:], func=ACT.Abs_reciprocal_sqrt, scale=1.0, bias=1.0)
+            nc.scalar.activation(out=a[:], in_=q_of[s][:], func=ACT.Abs_reciprocal_sqrt, scale=float(K * K), bias=K * K * SQ_EPS)
+            nc.scalar.activation(out=u[:], in_=g[:], func=ACT.Square)
+            small[s] = (a, u)
+
+        def norm_times(s):
+            t = work.tile([P, P], F32, name="norm")
+            engine = nc.gpsimd if ROUTE[s] == "Q" else nc.vector
+            engine.tensor_tensor(out=t[:], in0=q_of[s][:], in1=small[s][0][:], op=ALU.mult)
+            small[s] = (t, small[s][1])
+
+        def factor(s):
+            f = work.tile([P, P], F32, name="factor", bufs=4)
+            nc.gpsimd.tensor_tensor(out=f[:], in0=small[s][0][:], in1=small[s][1][:], op=ALU.mult)
+            small[s] = f
+
+        def scale_out(m, j0, j1):
+            s, c = divmod(m, QUADS)
+            h, t = STEPS[s]
+            if c == 0 and j0 == 0:
+                out_tiles[s] = work.tile([P, P, O], F32, name="out_tile", bufs=4)
+            nc.vector.tensor_tensor(
+                out=out_tiles[s][:, j0:j1, 4 * c:4 * c + 4],
+                in0=prod_banks[m][:].rearrange("p (o j) -> p j o", o=4)[:, j0:j1, :],
+                in1=small[s][:, j0:j1].unsqueeze(2).to_broadcast([P, j1 - j0, 4]),
+                op=ALU.mult,
+            )
+            if c == QUADS - 1:
+                nc.sync.dma_start(out=out2[t * P:(t + 1) * P, (h * P + j0) * O:(h * P + j1) * O],
+                                  in_=out_tiles[s][:, j0:j1, :].rearrange("p j o -> p (j o)"))
+
+        lag = {"D": DIRECT_LAG, "P": SUM_LAG, "Q": RED_LAG}
+        sum_slot = [QUADS * s + lag[ROUTE[s]] for s in range(len(STEPS))]
+        engine_of = {"s": "scalar", "v": "vector"}
+
+        turn_p(0, 7)
+        group_p(0, "scalar")
+        sort_w(0, 0, 8, 0, 16)
+        quantize_p(0)
+        sort_w(0, 0, 8, 16, 32)
+        sort_w(0, 8, 16, 0, 16)
+        for pair in range(8):
+            turn_w(0, pair, [3, 4, 5, 6, 7][pair % 5])
+            if pair == 1:
+                sort_w(0, 8, 16, 16, 32)
+            if pair in (3, 5, 7):
+                quantize_w(0, pair // 2 - 1)
+            group_w(0, pair, engine_of[HEAD_ENG[pair]])
+        turn_p(1, 6)
+        matmul_for_norm(0)
+        sort_w(1, 0, 8, 0, 16)
+        quantize_w(0, 3)
+        group_p(1, "vector")
+        square_and_add(0)
+        sort_w(1, 0, 8, 16, 32)
+        quantize_p(1)
+        sort_w(1, 8, 16, 0, 16)
+
+        prep = [("w", 0), ("w", 1), ("p", 2), ("p", 3), ("w", 2), ("w", 3), ("w", 4), ("w", 5), ("w", 6), ("w", 7)]
+        for slot in range(1, slots + OUT_LAG - QUADS):
+            if slot < slots:
+                matmul_for_norm(slot)
+            if slot >= OUT_LAG:
+                m = slot - OUT_LAG
+                prod_banks[m] = product_by_rows(m, OUT_BANKS[m % len(OUT_BANKS)])
+            for s in range(len(STEPS)):
+                if slot == sum_slot[s] + NORM_LAG:
+                    norm_times(s)
+                if slot == sum_slot[s] + FAC_LAG:
+                    factor(s)
+            if slot < slots:
+                square_and_add(slot)
+            if slot == 2:
+                sort_w(1, 8, 16, 16, 32)
+            if slot >= OUT_LAG:
+                scale_out(slot - OUT_LAG, 0, P)
+            for s in range(len(STEPS)):
+                if slot == sum_slot[s]:
+                    sum_squares(s)
+                if slot == sum_slot[s] + ROOT_LAG:
+                    roots(s)
+            for n, (kind, index) in enumerate(prep):
+                place = PREP_START + PREP_EVERY * (n // 2)
+                if slot == place:
+                    if kind == "p":
+                        turn_p(index, PREP_BANKS[n % 4])
+                    else:
+                        turn_w(1, index, PREP_BANKS[n % 4])
+                if slot == place + 1:
+                    if kind == "p":
+                        group_p(index, engine_of[PREP_ENG[n]])
+                    else:
+                        group_w(1, index, engine_of[PREP_ENG[n]])
+                if slot == place + 2:
+                    if kind == "p":
+                        quantize_p(index)
+                    elif index % 2 == 1:
+                        quantize_w(1, index // 2)
+        for m in range(slots - QUADS, slots):
+            prod_banks[m] = product_by_rows(m, LATE_NORM_BANKS[m % 4])
+        for j0 in range(0, P, P // TAIL_SPLIT):
+            for m in range(slots - QUADS, slots):
+                scale_out(m, j0, j0 + P // TAIL_SPLIT)

@@ -19,29 +19,45 @@ P = 128
 QUADS = 4
 TILES = B // P
 HALVES = K // P
-STEPS = [(h, t) for h in range(HALVES) for t in range(TILES)]
-ROUTE = "DPPQPPQPPQPPQPPD"
-SUM_LAG = 7
-DIRECT_LAG = 5
-RED_LAG = 8
+DIRECT_HEAD = []
+SUM_LAG = 4
+DIRECT_LAG = 2
 ROOT_LAG = 1
 NORM_LAG = 2
 FAC_LAG = 3
-OUT_LAG = 15
-NORM_BANKS = [0, 1, 2]
-LATE_NORM_BANKS = [0, 1, 2, 6]
+OUT_LAG = 6
+FIRST_OUT = 16
+CATCH_UP = 8
+NORM_BANKS = [0, 1, 2, 6]
 OUT_BANKS = [3, 4, 5]
-PREP_BANKS = [3, 4, 5, 6]
+PREP_BANKS = [3, 4, 5]
 Q_BANK = 7
-PREP_START = 4
-PREP_EVERY = 2
-HEAD_ENG = "svsvsvsv"
-PREP_ENG = "vsvsvsvsvsv"
+PREP_START = 1
+PREP_EVERY = 4
+RUN = 3
+HEAD_ENG = "ssssssss"
+PREP_ENG = "vsv"
 TAIL_SPLIT = 2
+WARM = 0
+AFTER = 1
+U_ON_G = 1
+TAILQ = 0
+V_ADDS = 8
+V_ADD_LAG = 1.6
+SPLIT_T = 2
+B_KEY = -0.1
+SINGLE_LAG = 3
+P_FIRST = 0
+SORT_FROM = 0
+FINE = 1
+SINGLES = 2
+NDIRECT = 1
 
 
 def tile_capsulenetwork_pb_kernel(tc, p, Wr, out):
     nc = tc.nc
+    STEPS = [(h, t, 2) for h in range(2) for t in range(0, 8, 2)][:8 - SINGLES // 2] + [(1, t, 1) for t in range(8 - SINGLES, 8)]
+    DIRECT = DIRECT_HEAD + list(range(len(STEPS) - NDIRECT, len(STEPS)))
     p2 = p.rearrange("(t b) n i -> b t (n i)", b=P)
     out2 = out.rearrange("b j o -> b (j o)")
 
@@ -62,9 +78,12 @@ def tile_capsulenetwork_pb_kernel(tc, p, Wr, out):
             nc.sync.dma_start(out=t[:], in_=Wr[n0:n1, h * P:(h + 1) * P, o0:o1, :].rearrange("n j o i -> j n (o i)"))
             w_raw[(h, o0, n0)] = t
 
-        nc.sync.dma_start(out=p_raw[:, 0:2, :], in_=p2[:, 0:2, :])
+        if P_FIRST:
+            nc.sync.dma_start(out=p_raw[:, 0:2, :], in_=p2[:, 0:2, :])
         load_w(0, 0, 8, 0, 16)
         load_w(0, 0, 8, 16, 32)
+        if not P_FIRST:
+            nc.sync.dma_start(out=p_raw[:, 0:2, :], in_=p2[:, 0:2, :])
         load_w(0, 8, 16, 0, 16)
         load_w(0, 8, 16, 16, 32)
         nc.sync.dma_start(out=p_raw[:, 2:4, :], in_=p2[:, 2:4, :])
@@ -133,177 +152,211 @@ def tile_capsulenetwork_pb_kernel(tc, p, Wr, out):
         def quantize_p(g):
             nc.vector.quantize_mx(out=p_codes[g][:].bitcast(FP8X4), scales=p_scales[g][:], in_=grouped[("p", g)][:])
 
-        slots = len(STEPS) * QUADS
+        norm_slots = [(s, k) for s, (h, t0, nb) in enumerate(STEPS) for k in range(QUADS * nb)]
+        out_slots = [(s, t0 + i, c) for s, (h, t0, nb) in enumerate(STEPS) for i in range(nb) for c in range(QUADS)]
+        slots = len(norm_slots)
+        last = len(STEPS) - 1
+        sum_slot = {s: slot + (DIRECT_LAG if s in DIRECT else SUM_LAG if STEPS[s][2] == 2 else SINGLE_LAG) for slot, (s, k) in enumerate(norm_slots)}
         norm_banks = {}
         squares = {}
         parts = {s: [] for s in range(len(STEPS))}
-        pair_tiles = {}
         q_of = {}
         small = {}
         out_tiles = {}
         prod_banks = {}
 
-        def p_operand(t):
-            cols = slice((t % 2) * P, (t % 2 + 1) * P)
-            return p_codes[t // 2][:, cols].bitcast(FP8X4), p_scales[t // 2][:, cols]
-
-        def product_by_rows(slot, bank_index):
-            s, c = divmod(slot, QUADS)
-            h, t = STEPS[s]
-            acc = bank(bank_index, [P, 4 * P])
-            codes, scales = p_operand(t)
-            nc.tensor.matmul_mx(out=acc[:], lhsT=codes, lhsT_scale=scales, rhs=w_codes[h][c][:].bitcast(FP8X4),
-                                rhs_scale=w_scales[h][c][:], start=True, stop=True)
-            return acc
+        def p_operand(t0, nb):
+            cols = slice((t0 % 2) * P, (t0 % 2 + nb) * P)
+            return p_codes[t0 // 2][:, cols].bitcast(FP8X4), p_scales[t0 // 2][:, cols]
 
         def matmul_for_norm(slot):
-            s, c = divmod(slot, QUADS)
-            h, t = STEPS[s]
-            banks = NORM_BANKS if slot < OUT_LAG else LATE_NORM_BANKS
-            bank_index = banks[slot % len(banks)]
-            if ROUTE[s] == "Q":
-                norm_banks[slot] = product_by_rows(slot, bank_index)
-                return
-            acc = bank(bank_index, [P, 4 * P])
-            codes, scales = p_operand(t)
-            for i in range(4):
-                cols = slice(i * P, (i + 1) * P)
-                nc.tensor.matmul_mx(out=acc[:, cols], lhsT=w_codes[h][c][:, cols].bitcast(FP8X4), lhsT_scale=w_scales[h][c][:, cols],
+            s, k = norm_slots[slot]
+            h, t0, nb = STEPS[s]
+            per_bank = 4 // nb
+            banks = NORM_BANKS
+            acc = bank(banks[slot % len(banks)], [P, per_bank, nb * P])
+            codes, scales = p_operand(t0, nb)
+            for i in range(per_bank):
+                c, o4 = divmod(k * per_bank + i, 4)
+                cols = slice(o4 * P, (o4 + 1) * P)
+                nc.tensor.matmul_mx(out=acc[:, i, :], lhsT=w_codes[h][c][:, cols].bitcast(FP8X4), lhsT_scale=w_scales[h][c][:, cols],
                                     rhs=codes, rhs_scale=scales, start=True, stop=True)
             norm_banks[slot] = acc
 
-        def square_and_add(slot):
-            s, c = divmod(slot, QUADS)
-            sq = work.tile([P, 4 * P], F32, name="sq", bufs=8)
-            if ROUTE[s] == "Q":
-                nc.scalar.activation(out=sq[:].rearrange("p (j o) -> p j o", o=4), in_=norm_banks[slot][:].rearrange("p (o j) -> p j o", o=4),
-                                     func=ACT.Square, scale=1.0 / K)
-            else:
-                nc.scalar.activation(out=sq[:], in_=norm_banks[slot][:], func=ACT.Square, scale=1.0 / K)
+        def square(slot):
+            sq = work.tile([P, 4, P], F32, name="sq", bufs=12)
+            nc.scalar.activation(out=sq[:].rearrange("p x b -> p (x b)"), in_=norm_banks[slot][:].rearrange("p o b -> p (o b)"), func=ACT.Square, scale=1.0 / K)
             squares[slot] = sq
-            if ROUTE[s] == "D":
-                parts[s].append(sq[:])
-            elif c % 2 == 1:
-                if c == 1:
-                    pair_tiles[s] = work.tile([P, 2, 4 * P], F32, name="pair_sum", bufs=4)
-                nc.gpsimd.tensor_tensor(out=pair_tiles[s][:, c // 2, :], in0=squares[slot - 1][:], in1=sq[:], op=ALU.add)
-                parts[s].append(pair_tiles[s][:, c // 2, :])
+            if norm_slots[slot][0] in DIRECT:
+                parts[norm_slots[slot][0]].append(sq)
 
-        def sum_squares(s):
-            if ROUTE[s] == "Q":
-                q = work.tile([P, P], F32, name="q_sbuf")
-                nc.vector.tensor_reduce(out=q[:], in_=pair_tiles[s][:].rearrange("p a (j o) -> p j a o", o=4), axis=mybir.AxisListType.XY, op=ALU.add)
-            else:
-                q = bank(Q_BANK, [P, P])
-                blocks = [part[:, x * P:(x + 1) * P] for part in parts[s] for x in range(4)]
-                for n, block in enumerate(blocks):
-                    nc.tensor.matmul(out=q[:], lhsT=block, rhs=ident[:], is_transpose=True, start=(n == 0), stop=(n == len(blocks) - 1))
-            q_of[s] = q
+        def add_pair(slot):
+            total = work.tile([P, 4, P], F32, name="pair_sum", bufs=10)
+            engine = nc.vector if slot < V_ADDS else nc.gpsimd
+            engine.tensor_tensor(out=total[:], in0=squares[slot - 1][:], in1=squares[slot][:], op=ALU.add)
+            parts[norm_slots[slot][0]].append(total)
+
+        def sum_squares(s, half, halves):
+            nb = STEPS[s][2]
+            if half == 0:
+                q_of[s] = bank(Q_BANK if s != last else TAILQ, [P, nb, P])
+            count = (4 if s in DIRECT else 2) * nb
+            for i in range(half * count // halves, (half + 1) * count // halves):
+                for x in range(4):
+                    nc.tensor.matmul(out=q_of[s][:, x % nb, :], lhsT=parts[s][i][:, x, :], rhs=ident[:], is_transpose=True,
+                                     start=(i == 0 and x == 0), stop=(i == count - 1 and x == 3))
 
         def roots(s):
-            a = work.tile([P, P], F32, name="inv_norm")
-            g = work.tile([P, P], F32, name="inv_root")
-            u = work.tile([P, P], F32, name="inv_one_plus")
+            nb = STEPS[s][2]
+            a = work.tile([P, nb, P], F32, name="inv_norm")
+            g = work.tile([P, nb, P], F32, name="inv_root")
+            u = work.tile([P, nb, P], F32, name="inv_one_plus")
             nc.scalar.activation(out=g[:], in_=q_of[s][:], func=ACT.Abs_reciprocal_sqrt, scale=1.0, bias=1.0)
             nc.scalar.activation(out=a[:], in_=q_of[s][:], func=ACT.Abs_reciprocal_sqrt, scale=float(K * K), bias=K * K * SQ_EPS)
-            nc.scalar.activation(out=u[:], in_=g[:], func=ACT.Square)
+            if U_ON_G and s not in DIRECT and s > 0:
+                nc.gpsimd.tensor_tensor(out=u[:], in0=g[:], in1=g[:], op=ALU.mult)
+            else:
+                nc.scalar.activation(out=u[:], in_=g[:], func=ACT.Square)
             small[s] = (a, u)
 
         def norm_times(s):
-            t = work.tile([P, P], F32, name="norm")
-            engine = nc.gpsimd if ROUTE[s] == "Q" else nc.vector
-            engine.tensor_tensor(out=t[:], in0=q_of[s][:], in1=small[s][0][:], op=ALU.mult)
+            t = work.tile([P, STEPS[s][2], P], F32, name="norm")
+            nc.vector.tensor_tensor(out=t[:], in0=q_of[s][:], in1=small[s][0][:], op=ALU.mult)
             small[s] = (t, small[s][1])
 
         def factor(s):
-            f = work.tile([P, P], F32, name="factor", bufs=4)
-            nc.gpsimd.tensor_tensor(out=f[:], in0=small[s][0][:], in1=small[s][1][:], op=ALU.mult)
+            f = work.tile([P, STEPS[s][2], P], F32, name="factor", bufs=4)
+            engine = nc.vector if s in DIRECT or s == 0 else nc.gpsimd
+            engine.tensor_tensor(out=f[:], in0=small[s][0][:], in1=small[s][1][:], op=ALU.mult)
             small[s] = f
 
+        def matmul_for_out(m, bank_index):
+            s, t, c = out_slots[m]
+            h = STEPS[s][0]
+            acc = bank(bank_index, [P, 4 * P])
+            codes, scales = p_operand(t, 1)
+            nc.tensor.matmul_mx(out=acc[:], lhsT=codes, lhsT_scale=scales, rhs=w_codes[h][c][:].bitcast(FP8X4),
+                                rhs_scale=w_scales[h][c][:], start=True, stop=True)
+            prod_banks[m] = acc
+
         def scale_out(m, j0, j1):
-            s, c = divmod(m, QUADS)
-            h, t = STEPS[s]
+            s, t, c = out_slots[m]
+            h, t0, nb = STEPS[s]
             if c == 0 and j0 == 0:
-                out_tiles[s] = work.tile([P, P, O], F32, name="out_tile", bufs=4)
+                out_tiles[(h, t)] = work.tile([P, P, O], F32, name="out_tile", bufs=4)
             nc.vector.tensor_tensor(
-                out=out_tiles[s][:, j0:j1, 4 * c:4 * c + 4],
+                out=out_tiles[(h, t)][:, j0:j1, 4 * c:4 * c + 4],
                 in0=prod_banks[m][:].rearrange("p (o j) -> p j o", o=4)[:, j0:j1, :],
-                in1=small[s][:, j0:j1].unsqueeze(2).to_broadcast([P, j1 - j0, 4]),
+                in1=small[s][:, t - t0, j0:j1].unsqueeze(2).to_broadcast([P, j1 - j0, 4]),
                 op=ALU.mult,
             )
             if c == QUADS - 1:
                 nc.sync.dma_start(out=out2[t * P:(t + 1) * P, (h * P + j0) * O:(h * P + j1) * O],
-                                  in_=out_tiles[s][:, j0:j1, :].rearrange("p j o -> p (j o)"))
+                                  in_=out_tiles[(h, t)][:, j0:j1, :].rearrange("p j o -> p (j o)"))
 
-        lag = {"D": DIRECT_LAG, "P": SUM_LAG, "Q": RED_LAG}
-        sum_slot = [QUADS * s + lag[ROUTE[s]] for s in range(len(STEPS))]
+        def square_and_add(slot):
+            square(slot)
+            if slot % 2 == 1 and norm_slots[slot][0] not in DIRECT:
+                add_pair(slot)
+
         engine_of = {"s": "scalar", "v": "vector"}
+        if WARM:
+            zeros = keep.tile([P, 4 * P], BF16, name="zeros")
+            nc.vector.memset(zeros[:], 0.0)
+            scratch = bank(0, [P, 4 * P])
+            for n in range(WARM):
+                nc.tensor.matmul(out=scratch[:], lhsT=zeros[:, 0:P], rhs=zeros[:], start=True, stop=True)
 
-        turn_p(0, 7)
-        group_p(0, "scalar")
+        w1_chunks = [(0, 8, 0, 16), (0, 8, 16, 32), (8, 16, 0, 16), (8, 16, 16, 32)]
+        if P_FIRST:
+            turn_p(0, 0)
+            group_p(0, "scalar")
         sort_w(0, 0, 8, 0, 16)
-        quantize_p(0)
+        if P_FIRST:
+            quantize_p(0)
         sort_w(0, 0, 8, 16, 32)
+        if not P_FIRST:
+            turn_p(0, 0)
+            group_p(0, "scalar")
         sort_w(0, 8, 16, 0, 16)
+        if not P_FIRST:
+            quantize_p(0)
+        sort_w(0, 8, 16, 16, 32)
         for pair in range(8):
-            turn_w(0, pair, [3, 4, 5, 6, 7][pair % 5])
-            if pair == 1:
-                sort_w(0, 8, 16, 16, 32)
-            if pair in (3, 5, 7):
-                quantize_w(0, pair // 2 - 1)
+            turn_w(0, pair, [3, 4, 5, 6, 7, 1, 2][pair % 7])
             group_w(0, pair, engine_of[HEAD_ENG[pair]])
-        turn_p(1, 6)
-        matmul_for_norm(0)
-        sort_w(1, 0, 8, 0, 16)
-        quantize_w(0, 3)
-        group_p(1, "vector")
-        square_and_add(0)
-        sort_w(1, 0, 8, 16, 32)
-        quantize_p(1)
-        sort_w(1, 8, 16, 0, 16)
+            if pair % 2 == 1:
+                quantize_w(0, pair // 2)
+                if pair // 2 >= SORT_FROM:
+                    sort_w(1, *w1_chunks[pair // 2 - SORT_FROM])
+        for chunk in w1_chunks[4 - SORT_FROM:]:
+            sort_w(1, *chunk)
 
-        prep = [("w", 0), ("w", 1), ("p", 2), ("p", 3), ("w", 2), ("w", 3), ("w", 4), ("w", 5), ("w", 6), ("w", 7)]
-        for slot in range(1, slots + OUT_LAG - QUADS):
-            if slot < slots:
-                matmul_for_norm(slot)
-            if slot >= OUT_LAG:
-                m = slot - OUT_LAG
-                prod_banks[m] = product_by_rows(m, OUT_BANKS[m % len(OUT_BANKS)])
-            for s in range(len(STEPS)):
-                if slot == sum_slot[s] + NORM_LAG:
-                    norm_times(s)
-                if slot == sum_slot[s] + FAC_LAG:
-                    factor(s)
-            if slot < slots:
-                square_and_add(slot)
-            if slot == 2:
-                sort_w(1, 8, 16, 16, 32)
-            if slot >= OUT_LAG:
-                scale_out(slot - OUT_LAG, 0, P)
-            for s in range(len(STEPS)):
-                if slot == sum_slot[s]:
-                    sum_squares(s)
-                if slot == sum_slot[s] + ROOT_LAG:
-                    roots(s)
-            for n, (kind, index) in enumerate(prep):
-                place = PREP_START + PREP_EVERY * (n // 2)
-                if slot == place:
-                    if kind == "p":
-                        turn_p(index, PREP_BANKS[n % 4])
-                    else:
-                        turn_w(1, index, PREP_BANKS[n % 4])
-                if slot == place + 1:
-                    if kind == "p":
-                        group_p(index, engine_of[PREP_ENG[n]])
-                    else:
-                        group_w(1, index, engine_of[PREP_ENG[n]])
-                if slot == place + 2:
-                    if kind == "p":
-                        quantize_p(index)
-                    elif index % 2 == 1:
-                        quantize_w(1, index // 2)
-        for m in range(slots - QUADS, slots):
-            prod_banks[m] = product_by_rows(m, LATE_NORM_BANKS[m % 4])
-        for j0 in range(0, P, P // TAIL_SPLIT):
-            for m in range(slots - QUADS, slots):
-                scale_out(m, j0, j0 + P // TAIL_SPLIT)
+        prep = [("p", 1), ("w", 0), ("w", 1), ("w", 2), ("w", 3), ("p", 2), ("w", 4), ("w", 5), ("p", 3), ("w", 6), ("w", 7)]
+        events = []
+
+        def at(key, call, *args):
+            events.append((key, len(events), call, args))
+
+        sums = set(sum_slot.values())
+        for slot in range(slots):
+            key = slot
+            for back in range(1, AFTER):
+                if slot - back - 1 in sums:
+                    key = slot - back + 0.01 * back
+            if slot in sums:
+                key = slot + 0.15
+            at(key, matmul_for_norm, slot)
+            at(slot + 0.5, square, slot)
+            if slot % 2 == 1 and norm_slots[slot][0] not in DIRECT:
+                at(slot + (V_ADD_LAG if slot < V_ADDS else 0.55), add_pair, slot)
+        for s in range(len(STEPS)):
+            halves = SPLIT_T if STEPS[s][2] == 2 else (2 if s == last else 1)
+            for half in range(halves):
+                at(sum_slot[s] - (halves - 1 - half) * QUADS * STEPS[s][2] // halves + 0.8, sum_squares, s, half, halves)
+            at(sum_slot[s] + ROOT_LAG + 0.3, roots, s)
+            at(sum_slot[s] + NORM_LAG + 0.3, norm_times, s)
+            at(sum_slot[s] + FAC_LAG + 0.6, factor, s)
+        slot = FIRST_OUT
+        m = 0
+        while m < len(out_slots) - QUADS * FINE:
+            for extra in range(2 if slot % CATCH_UP == 0 else 1):
+                if m < len(out_slots) - QUADS * FINE and slot >= sum_slot[out_slots[m][0]] + OUT_LAG:
+                    at(slot + B_KEY, matmul_for_out, m, OUT_BANKS[m % len(OUT_BANKS)])
+                    at(slot + 0.7, scale_out, m, 0, P)
+                    m += 1
+            slot += 1
+
+        def turn(kind, index, bank_index):
+            if kind == "p":
+                turn_p(index, bank_index)
+            else:
+                turn_w(1, index, bank_index)
+
+        def group(kind, index, engine):
+            if kind == "p":
+                group_p(index, engine)
+            else:
+                group_w(1, index, engine)
+
+        def quantize(kind, index):
+            if kind == "p":
+                quantize_p(index)
+            elif index % 2 == 1:
+                quantize_w(1, index // 2)
+
+        for n, (kind, index) in enumerate(prep):
+            place = PREP_START + PREP_EVERY * (n // RUN)
+            at(place + 0.85, turn, kind, index, PREP_BANKS[n % RUN])
+            at(place + 0.9, group, kind, index, engine_of[PREP_ENG[n % RUN]])
+            at(place + 0.95, quantize, kind, index)
+        for key, order, call, args in sorted(events, key=lambda e: e[:2]):
+            call(*args)
+        for first in range(len(out_slots) - QUADS * FINE, len(out_slots), QUADS):
+            spare = [7, 1, 2, 6] if first == len(out_slots) - QUADS * FINE else [0, 3, 4, 5]
+            for m in range(first, first + QUADS):
+                matmul_for_out(m, spare[m % 4])
+            split = TAIL_SPLIT if first == len(out_slots) - QUADS else 2
+            for j0 in range(0, P, P // split):
+                for m in range(first, first + QUADS):
+                    scale_out(m, j0, j0 + P // split)

@@ -19,14 +19,16 @@ P = 128
 QUADS = 4
 TILES = B // P
 HALVES = K // P
-DIRECT_HEAD = []
+PLAN = "T2 T2 T2 T2 T2 T2 T2 T1 D1"
 SUM_LAG = 4
+SINGLE_LAG = 4
 DIRECT_LAG = 2
+RED_LAG = 2
 ROOT_LAG = 1
 NORM_LAG = 2
-FAC_LAG = 3
+FAC_LAG = 2
 OUT_LAG = 6
-FIRST_OUT = 16
+FIRST_OUT = 17
 CATCH_UP = 8
 NORM_BANKS = [0, 1, 2, 6]
 OUT_BANKS = [3, 4, 5]
@@ -39,25 +41,28 @@ HEAD_ENG = "ssssssss"
 PREP_ENG = "vsv"
 TAIL_SPLIT = 2
 WARM = 0
-AFTER = 1
-U_ON_G = 1
+U_ON_G = 0
 TAILQ = 0
-V_ADDS = 8
+V_ADDS = 12
 V_ADD_LAG = 1.6
-SPLIT_T = 2
 B_KEY = -0.1
-SINGLE_LAG = 3
-P_FIRST = 0
-SORT_FROM = 0
-FINE = 1
-SINGLES = 2
-NDIRECT = 1
+P_FIRST = 1
+SORT_AT = [1, 3, 5, 7]
+GB = 1
+G_TILE = -1
+G_KEY = 66
+FAC_KEY = 0.52
 
 
 def tile_capsulenetwork_pb_kernel(tc, p, Wr, out):
     nc = tc.nc
-    STEPS = [(h, t, 2) for h in range(2) for t in range(0, 8, 2)][:8 - SINGLES // 2] + [(1, t, 1) for t in range(8 - SINGLES, 8)]
-    DIRECT = DIRECT_HEAD + list(range(len(STEPS) - NDIRECT, len(STEPS)))
+    STEPS = []
+    ROUTE = []
+    tile_at = 0
+    for word in PLAN.split():
+        STEPS.append((tile_at // TILES, tile_at % TILES, int(word[1])))
+        ROUTE.append(word[0])
+        tile_at += int(word[1])
     p2 = p.rearrange("(t b) n i -> b t (n i)", b=P)
     out2 = out.rearrange("b j o -> b (j o)")
 
@@ -80,17 +85,13 @@ def tile_capsulenetwork_pb_kernel(tc, p, Wr, out):
 
         if P_FIRST:
             nc.sync.dma_start(out=p_raw[:, 0:2, :], in_=p2[:, 0:2, :])
-        load_w(0, 0, 8, 0, 16)
-        load_w(0, 0, 8, 16, 32)
+        for n0 in range(0, N, 8):
+            load_w(0, 0, 16, n0, n0 + 8)
         if not P_FIRST:
             nc.sync.dma_start(out=p_raw[:, 0:2, :], in_=p2[:, 0:2, :])
-        load_w(0, 8, 16, 0, 16)
-        load_w(0, 8, 16, 16, 32)
         nc.sync.dma_start(out=p_raw[:, 2:4, :], in_=p2[:, 2:4, :])
-        load_w(1, 0, 8, 0, 16)
-        load_w(1, 0, 8, 16, 32)
-        load_w(1, 8, 16, 0, 16)
-        load_w(1, 8, 16, 16, 32)
+        for n0 in range(0, N, 8):
+            load_w(1, 0, 16, n0, n0 + 8)
         nc.sync.dma_start(out=p_raw[:, 4:TILES, :], in_=p2[:, 4:TILES, :])
 
         ident = keep.tile([P, P], F32, name="ident")
@@ -99,14 +100,14 @@ def tile_capsulenetwork_pb_kernel(tc, p, Wr, out):
         w_sorted = [keep.tile([P, O, 2, N, 4], F32, name="w_sorted%d" % h, align_bytes=64) for h in range(HALVES)]
         w_codes = [[keep.tile([P, 4 * P], U32, name="w_codes%d_%d" % (h, c), align_bytes=64) for c in range(QUADS)] for h in range(HALVES)]
         w_scales = [[keep.tile([P, 4 * P], U8, name="w_scales%d_%d" % (h, c), align_bytes=64) for c in range(QUADS)] for h in range(HALVES)]
-        p_codes = [keep.tile([P, 2 * P], U32, name="p_codes%d" % g, align_bytes=64) for g in range(TILES // 2)]
-        p_scales = [keep.tile([P, 2 * P], U8, name="p_scales%d" % g, align_bytes=64) for g in range(TILES // 2)]
+        p_codes = keep.tile([P, B], U32, name="p_codes", align_bytes=64)
+        p_scales = keep.tile([P, B], U8, name="p_scales", align_bytes=64)
 
-        def sort_w(h, o0, o1, n0, n1):
-            src = w_raw[(h, o0, n0)][:].rearrange("p n x -> p (n x)").bitcast(F32)
+        def sort_w(h, n0, o0=0, o1=O):
+            src = w_raw[(h, 0, n0)][:].rearrange("p n x -> p (n x)").bitcast(F32)
             nc.vector.tensor_copy(
-                out=w_sorted[h][:, o0:o1, :, n0:n1, :],
-                in_=src.rearrange("p (n o i u) -> p o u n i", n=n1 - n0, i=4, u=2),
+                out=w_sorted[h][:, o0:o1, :, n0:n0 + 8, :],
+                in_=src.rearrange("p (n o i u) -> p o u n i", n=8, i=4, u=2)[:, o0:o1],
             )
 
         turned = {}
@@ -150,15 +151,16 @@ def tile_capsulenetwork_pb_kernel(tc, p, Wr, out):
             nc.vector.quantize_mx(out=w_codes[h][c][:].bitcast(FP8X4), scales=w_scales[h][c][:], in_=grouped[("w", h, c)][:])
 
         def quantize_p(g):
-            nc.vector.quantize_mx(out=p_codes[g][:].bitcast(FP8X4), scales=p_scales[g][:], in_=grouped[("p", g)][:])
+            nc.vector.quantize_mx(out=p_codes[:, 2 * g * P:2 * (g + 1) * P].bitcast(FP8X4), scales=p_scales[:, 2 * g * P:2 * (g + 1) * P], in_=grouped[("p", g)][:])
 
         norm_slots = [(s, k) for s, (h, t0, nb) in enumerate(STEPS) for k in range(QUADS * nb)]
         out_slots = [(s, t0 + i, c) for s, (h, t0, nb) in enumerate(STEPS) for i in range(nb) for c in range(QUADS)]
         slots = len(norm_slots)
         last = len(STEPS) - 1
-        sum_slot = {s: slot + (DIRECT_LAG if s in DIRECT else SUM_LAG if STEPS[s][2] == 2 else SINGLE_LAG) for slot, (s, k) in enumerate(norm_slots)}
+        sum_slot = {s: slot + {"D1": DIRECT_LAG, "T2": SUM_LAG, "T1": SINGLE_LAG, "V1": RED_LAG + 3, "D2": DIRECT_LAG}[PLAN.split()[s]] for slot, (s, k) in enumerate(norm_slots)}
         norm_banks = {}
         squares = {}
+        totals = {}
         parts = {s: [] for s in range(len(STEPS))}
         q_of = {}
         small = {}
@@ -166,14 +168,24 @@ def tile_capsulenetwork_pb_kernel(tc, p, Wr, out):
         prod_banks = {}
 
         def p_operand(t0, nb):
-            cols = slice((t0 % 2) * P, (t0 % 2 + nb) * P)
-            return p_codes[t0 // 2][:, cols].bitcast(FP8X4), p_scales[t0 // 2][:, cols]
+            cols = slice(t0 * P, (t0 + nb) * P)
+            return p_codes[:, cols].bitcast(FP8X4), p_scales[:, cols]
+
+        def by_rows(h, t, c, bank_index):
+            acc = bank(bank_index, [P, 4 * P])
+            codes, scales = p_operand(t, 1)
+            nc.tensor.matmul_mx(out=acc[:], lhsT=codes, lhsT_scale=scales, rhs=w_codes[h][c][:].bitcast(FP8X4),
+                                rhs_scale=w_scales[h][c][:], start=True, stop=True)
+            return acc
 
         def matmul_for_norm(slot):
             s, k = norm_slots[slot]
             h, t0, nb = STEPS[s]
             per_bank = 4 // nb
             banks = NORM_BANKS
+            if ROUTE[s] == "V":
+                norm_banks[slot] = by_rows(h, t0, k, banks[slot % len(banks)])
+                return
             acc = bank(banks[slot % len(banks)], [P, per_bank, nb * P])
             codes, scales = p_operand(t0, nb)
             for i in range(per_bank):
@@ -184,27 +196,47 @@ def tile_capsulenetwork_pb_kernel(tc, p, Wr, out):
             norm_banks[slot] = acc
 
         def square(slot):
-            sq = work.tile([P, 4, P], F32, name="sq", bufs=12)
-            nc.scalar.activation(out=sq[:].rearrange("p x b -> p (x b)"), in_=norm_banks[slot][:].rearrange("p o b -> p (o b)"), func=ACT.Square, scale=1.0 / K)
-            squares[slot] = sq
-            if norm_slots[slot][0] in DIRECT:
-                parts[norm_slots[slot][0]].append(sq)
+            s, k = norm_slots[slot]
+            if slot % 4 == 0:
+                squares[slot // 4] = work.tile([P, 4, 4 * P], F32, name="sq", bufs=4)
+            sq = squares[slot // 4]
+            if ROUTE[s] == "V":
+                dst = sq[:].rearrange("p a x -> p (a x)").rearrange("p (j o) -> p j o", o=O)[:, :, 4 * k:4 * k + 4]
+                nc.scalar.activation(out=dst, in_=norm_banks[slot][:].rearrange("p (o j) -> p j o", o=4), func=ACT.Square, scale=1.0 / K)
+                return
+            nc.scalar.activation(out=sq[:, slot % 4, :], in_=norm_banks[slot][:].rearrange("p o b -> p (o b)"), func=ACT.Square, scale=1.0 / K)
+            if ROUTE[s] == "D":
+                parts[s].append(sq[:, slot % 4, :])
 
-        def add_pair(slot):
-            total = work.tile([P, 4, P], F32, name="pair_sum", bufs=10)
+        def add_pair(slot, count):
+            sq = squares[slot // 4]
+            if slot % 4 == 2 * count - 1:
+                totals[slot // 4] = work.tile([P, 2, 4 * P], F32, name="pair_sum", bufs=4)
+            total = totals[slot // 4]
             engine = nc.vector if slot < V_ADDS else nc.gpsimd
-            engine.tensor_tensor(out=total[:], in0=squares[slot - 1][:], in1=squares[slot][:], op=ALU.add)
-            parts[norm_slots[slot][0]].append(total)
+            if count == 2:
+                engine.tensor_tensor(out=total[:], in0=sq[:, 0:2, :], in1=sq[:, 2:4, :], op=ALU.add)
+                parts[norm_slots[slot][0]].extend([total[:, 0, :], total[:, 1, :]])
+            else:
+                a = (slot % 4) // 2
+                engine.tensor_tensor(out=total[:, a, :], in0=sq[:, 2 * a, :], in1=sq[:, 2 * a + 1, :], op=ALU.add)
+                parts[norm_slots[slot][0]].append(total[:, a, :])
 
         def sum_squares(s, half, halves):
             nb = STEPS[s][2]
             if half == 0:
                 q_of[s] = bank(Q_BANK if s != last else TAILQ, [P, nb, P])
-            count = (4 if s in DIRECT else 2) * nb
+            count = (4 if ROUTE[s] == "D" else 2) * nb
             for i in range(half * count // halves, (half + 1) * count // halves):
                 for x in range(4):
-                    nc.tensor.matmul(out=q_of[s][:, x % nb, :], lhsT=parts[s][i][:, x, :], rhs=ident[:], is_transpose=True,
+                    nc.tensor.matmul(out=q_of[s][:, x % nb, :], lhsT=parts[s][i][:, x * P:(x + 1) * P], rhs=ident[:], is_transpose=True,
                                      start=(i == 0 and x == 0), stop=(i == count - 1 and x == 3))
+
+        def reduce_squares(s, first_slot, quarter):
+            if quarter == 0:
+                q_of[s] = work.tile([P, 1, P], F32, name="q_sbuf")
+            nc.vector.tensor_reduce(out=q_of[s][:, 0, quarter * 32:(quarter + 1) * 32], in_=squares[first_slot // 4][:, quarter, :].rearrange("p (j o) -> p j o", o=O),
+                                    axis=mybir.AxisListType.X, op=ALU.add)
 
         def roots(s):
             nb = STEPS[s][2]
@@ -213,7 +245,7 @@ def tile_capsulenetwork_pb_kernel(tc, p, Wr, out):
             u = work.tile([P, nb, P], F32, name="inv_one_plus")
             nc.scalar.activation(out=g[:], in_=q_of[s][:], func=ACT.Abs_reciprocal_sqrt, scale=1.0, bias=1.0)
             nc.scalar.activation(out=a[:], in_=q_of[s][:], func=ACT.Abs_reciprocal_sqrt, scale=float(K * K), bias=K * K * SQ_EPS)
-            if U_ON_G and s not in DIRECT and s > 0:
+            if U_ON_G and ROUTE[s] != "D" and s > 0:
                 nc.gpsimd.tensor_tensor(out=u[:], in0=g[:], in1=g[:], op=ALU.mult)
             else:
                 nc.scalar.activation(out=u[:], in_=g[:], func=ACT.Square)
@@ -221,23 +253,38 @@ def tile_capsulenetwork_pb_kernel(tc, p, Wr, out):
 
         def norm_times(s):
             t = work.tile([P, STEPS[s][2], P], F32, name="norm")
-            nc.vector.tensor_tensor(out=t[:], in0=q_of[s][:], in1=small[s][0][:], op=ALU.mult)
+            engine = nc.gpsimd if ROUTE[s] == "V" else nc.vector
+            engine.tensor_tensor(out=t[:], in0=q_of[s][:], in1=small[s][0][:], op=ALU.mult)
             small[s] = (t, small[s][1])
 
         def factor(s):
             f = work.tile([P, STEPS[s][2], P], F32, name="factor", bufs=4)
-            engine = nc.vector if s in DIRECT or s == 0 else nc.gpsimd
+            engine = nc.vector if s == 0 or (s == last and G_TILE < 0) else nc.gpsimd
             engine.tensor_tensor(out=f[:], in0=small[s][0][:], in1=small[s][1][:], op=ALU.mult)
             small[s] = f
 
         def matmul_for_out(m, bank_index):
             s, t, c = out_slots[m]
+            prod_banks[m] = by_rows(STEPS[s][0], t, c, bank_index)
+
+        def copy_out(m):
+            s, t, c = out_slots[m]
             h = STEPS[s][0]
-            acc = bank(bank_index, [P, 4 * P])
-            codes, scales = p_operand(t, 1)
-            nc.tensor.matmul_mx(out=acc[:], lhsT=codes, lhsT_scale=scales, rhs=w_codes[h][c][:].bitcast(FP8X4),
-                                rhs_scale=w_scales[h][c][:], start=True, stop=True)
-            prod_banks[m] = acc
+            if c == 0:
+                out_tiles[(h, t)] = work.tile([P, P, O], F32, name="plain_tile", bufs=1)
+            nc.scalar.copy(out=out_tiles[(h, t)][:, :, 4 * c:4 * c + 4], in_=prod_banks[m][:].rearrange("p (o j) -> p j o", o=4))
+
+        def scale_on_gpsimd(m, j0, j1):
+            s, t, c = out_slots[m]
+            h, t0, nb = STEPS[s]
+            part = out_tiles[(h, t)][:, j0:j1, :]
+            nc.gpsimd.tensor_tensor(out=part, in0=part, in1=small[s][:, t - t0, j0:j1].unsqueeze(2).to_broadcast([P, j1 - j0, O]), op=ALU.mult)
+
+        def store_part(m, j0, j1):
+            s, t, c = out_slots[m]
+            h = STEPS[s][0]
+            nc.sync.dma_start(out=out2[t * P:(t + 1) * P, (h * P + j0) * O:(h * P + j1) * O],
+                              in_=out_tiles[(h, t)][:, j0:j1, :].rearrange("p j o -> p (j o)"))
 
         def scale_out(m, j0, j1):
             s, t, c = out_slots[m]
@@ -254,11 +301,6 @@ def tile_capsulenetwork_pb_kernel(tc, p, Wr, out):
                 nc.sync.dma_start(out=out2[t * P:(t + 1) * P, (h * P + j0) * O:(h * P + j1) * O],
                                   in_=out_tiles[(h, t)][:, j0:j1, :].rearrange("p j o -> p (j o)"))
 
-        def square_and_add(slot):
-            square(slot)
-            if slot % 2 == 1 and norm_slots[slot][0] not in DIRECT:
-                add_pair(slot)
-
         engine_of = {"s": "scalar", "v": "vector"}
         if WARM:
             zeros = keep.tile([P, 4 * P], BF16, name="zeros")
@@ -267,30 +309,33 @@ def tile_capsulenetwork_pb_kernel(tc, p, Wr, out):
             for n in range(WARM):
                 nc.tensor.matmul(out=scratch[:], lhsT=zeros[:, 0:P], rhs=zeros[:], start=True, stop=True)
 
-        w1_chunks = [(0, 8, 0, 16), (0, 8, 16, 32), (8, 16, 0, 16), (8, 16, 16, 32)]
         if P_FIRST:
             turn_p(0, 0)
             group_p(0, "scalar")
-        sort_w(0, 0, 8, 0, 16)
+        sort_w(0, 0)
         if P_FIRST:
             quantize_p(0)
-        sort_w(0, 0, 8, 16, 32)
-        if not P_FIRST:
-            turn_p(0, 0)
-            group_p(0, "scalar")
-        sort_w(0, 8, 16, 0, 16)
-        if not P_FIRST:
-            quantize_p(0)
-        sort_w(0, 8, 16, 16, 32)
+        sort_w(0, 8)
+        sort_w(0, 16)
+        sort_w(0, 24, 0, 8)
+        sort_w(0, 24, 8, 16)
         for pair in range(8):
             turn_w(0, pair, [3, 4, 5, 6, 7, 1, 2][pair % 7])
+            if pair == 3 and not P_FIRST:
+                turn_p(0, 0)
             group_w(0, pair, engine_of[HEAD_ENG[pair]])
+            if pair == 3 and not P_FIRST:
+                group_p(0, "vector")
+            if pair == 4 and not P_FIRST:
+                quantize_p(0)
             if pair % 2 == 1:
                 quantize_w(0, pair // 2)
-                if pair // 2 >= SORT_FROM:
-                    sort_w(1, *w1_chunks[pair // 2 - SORT_FROM])
-        for chunk in w1_chunks[4 - SORT_FROM:]:
-            sort_w(1, *chunk)
+            for n in range(4):
+                if SORT_AT[n] == pair:
+                    sort_w(1, 8 * n)
+        for n in range(4):
+            if SORT_AT[n] == 8:
+                sort_w(1, 8 * n)
 
         prep = [("p", 1), ("w", 0), ("w", 1), ("w", 2), ("w", 3), ("p", 2), ("w", 4), ("w", 5), ("p", 3), ("w", 6), ("w", 7)]
         events = []
@@ -298,34 +343,41 @@ def tile_capsulenetwork_pb_kernel(tc, p, Wr, out):
         def at(key, call, *args):
             events.append((key, len(events), call, args))
 
-        sums = set(sum_slot.values())
         for slot in range(slots):
-            key = slot
-            for back in range(1, AFTER):
-                if slot - back - 1 in sums:
-                    key = slot - back + 0.01 * back
-            if slot in sums:
-                key = slot + 0.15
-            at(key, matmul_for_norm, slot)
+            s, k = norm_slots[slot]
+            at(slot, matmul_for_norm, slot)
             at(slot + 0.5, square, slot)
-            if slot % 2 == 1 and norm_slots[slot][0] not in DIRECT:
-                at(slot + (V_ADD_LAG if slot < V_ADDS else 0.55), add_pair, slot)
+            count = 1 if slot < V_ADDS else GB
+            if ROUTE[s] == "T" and slot % (2 * count) == 2 * count - 1:
+                at(slot + (V_ADD_LAG if slot < V_ADDS else 0.55), add_pair, slot, count)
+            if ROUTE[s] == "V" and k == 3:
+                for quarter in range(4):
+                    at(slot + RED_LAG + quarter + 0.75, reduce_squares, s, slot - 3, quarter)
         for s in range(len(STEPS)):
-            halves = SPLIT_T if STEPS[s][2] == 2 else (2 if s == last else 1)
-            for half in range(halves):
-                at(sum_slot[s] - (halves - 1 - half) * QUADS * STEPS[s][2] // halves + 0.8, sum_squares, s, half, halves)
+            halves = 2 if STEPS[s][2] == 2 or s == last else 1
+            if ROUTE[s] != "V":
+                for half in range(halves):
+                    at(sum_slot[s] - (halves - 1 - half) * QUADS * STEPS[s][2] // halves + 0.8, sum_squares, s, half, halves)
             at(sum_slot[s] + ROOT_LAG + 0.3, roots, s)
             at(sum_slot[s] + NORM_LAG + 0.3, norm_times, s)
-            at(sum_slot[s] + FAC_LAG + 0.6, factor, s)
+            at(sum_slot[s] + FAC_LAG + FAC_KEY, factor, s)
         slot = FIRST_OUT
-        m = 0
-        while m < len(out_slots) - QUADS * FINE:
+        todo = [m for m in range(len(out_slots) - QUADS) if m // QUADS != G_TILE]
+        n = 0
+        while n < len(todo):
             for extra in range(2 if slot % CATCH_UP == 0 else 1):
-                if m < len(out_slots) - QUADS * FINE and slot >= sum_slot[out_slots[m][0]] + OUT_LAG:
-                    at(slot + B_KEY, matmul_for_out, m, OUT_BANKS[m % len(OUT_BANKS)])
-                    at(slot + 0.7, scale_out, m, 0, P)
-                    m += 1
+                if n < len(todo) and slot >= sum_slot[out_slots[todo[n]][0]] + OUT_LAG:
+                    at(slot + B_KEY, matmul_for_out, todo[n], OUT_BANKS[n % len(OUT_BANKS)])
+                    at(slot + 0.7, scale_out, todo[n], 0, P)
+                    n += 1
             slot += 1
+        if G_TILE >= 0:
+            for c in range(QUADS):
+                at(slots + c, matmul_for_out, QUADS * G_TILE + c, NORM_BANKS[(slots + c + 1) % 4] if c < 3 else 1)
+                at(slots + c + 0.5, copy_out, QUADS * G_TILE + c)
+            for half in range(2):
+                at(G_KEY + 3 + 0.01 * half, scale_on_gpsimd, QUADS * G_TILE, half * 64, half * 64 + 64)
+                at(G_KEY + 6 + 4 * half, store_part, QUADS * G_TILE, half * 64, half * 64 + 64)
 
         def turn(kind, index, bank_index):
             if kind == "p":
@@ -352,11 +404,8 @@ def tile_capsulenetwork_pb_kernel(tc, p, Wr, out):
             at(place + 0.95, quantize, kind, index)
         for key, order, call, args in sorted(events, key=lambda e: e[:2]):
             call(*args)
-        for first in range(len(out_slots) - QUADS * FINE, len(out_slots), QUADS):
-            spare = [7, 1, 2, 6] if first == len(out_slots) - QUADS * FINE else [0, 3, 4, 5]
-            for m in range(first, first + QUADS):
-                matmul_for_out(m, spare[m % 4])
-            split = TAIL_SPLIT if first == len(out_slots) - QUADS else 2
-            for j0 in range(0, P, P // split):
-                for m in range(first, first + QUADS):
-                    scale_out(m, j0, j0 + P // split)
+        for m in range(len(out_slots) - QUADS, len(out_slots)):
+            matmul_for_out(m, [7, 1, 2, 6][m % 4])
+        for j0 in range(0, P, P // TAIL_SPLIT):
+            for m in range(len(out_slots) - QUADS, len(out_slots)):
+                scale_out(m, j0, j0 + P // TAIL_SPLIT)

@@ -16,55 +16,33 @@ ACT = mybir.ActivationFunctionType
 ALU = mybir.AluOpType
 
 P = 128
-QUADS = 4
-TILES = B // P
+BANK = 512
 HALVES = K // P
-PLAN = "T2 T2 T2 T2 T2 T2 T2 T1 D1"
+TILES = B // P
+GROUPS = TILES // 2
+QUADS = O // 4
+PAIRS = O // 2
+N_CHUNK = 8
+
+STEPS = HALVES * GROUPS
+STEP_SLOTS = PAIRS
+SLOTS = STEPS * STEP_SLOTS
+
 SUM_LAG = 4
-SINGLE_LAG = 4
-DIRECT_LAG = 2
-RED_LAG = 2
-ROOT_LAG = 1
-NORM_LAG = 2
-FAC_LAG = 2
-OUT_LAG = 6
-FIRST_OUT = 17
-CATCH_UP = 8
-NORM_BANKS = [0, 1, 2, 6]
-OUT_BANKS = [3, 4, 5]
-PREP_BANKS = [3, 4, 5]
+OUT_LAG = 10
+PREP_START = 4
+PREP_EVERY = 3
+VECTOR_ADD_STEPS = 2
+
+NORM_BANKS = (0, 1, 2, 6)
+OUT_BANKS = (3, 4, 5)
 Q_BANK = 7
-PREP_START = 1
-PREP_EVERY = 4
-RUN = 3
-HEAD_ENG = "ssssssss"
-PREP_ENG = "vsv"
-TAIL_SPLIT = 2
-WARM = 0
-U_ON_G = 0
-TAILQ = 0
-V_ADDS = 12
-V_ADD_LAG = 1.6
-B_KEY = -0.1
-P_FIRST = 1
-SORT_AT = [1, 3, 5, 7]
-GB = 1
-G_TILE = -1
-G_KEY = 66
-FAC_KEY = 0.52
 
 
 def tile_capsulenetwork_pb_kernel(tc, p, Wr, out):
     nc = tc.nc
-    STEPS = []
-    ROUTE = []
-    tile_at = 0
-    for word in PLAN.split():
-        STEPS.append((tile_at // TILES, tile_at % TILES, int(word[1])))
-        ROUTE.append(word[0])
-        tile_at += int(word[1])
-    p2 = p.rearrange("(t b) n i -> b t (n i)", b=P)
-    out2 = out.rearrange("b j o -> b (j o)")
+    p_rows = p.rearrange("(t b) n i -> b t (n i)", b=P)
+    out_rows = out.rearrange("b j o -> b (j o)")
 
     with ExitStack() as ctx:
         keep = ctx.enter_context(tc.tile_pool(name="keep", bufs=1))
@@ -78,334 +56,257 @@ def tile_capsulenetwork_pb_kernel(tc, p, Wr, out):
         p_raw = keep.tile([P, TILES, N * I], BF16, name="p_raw", align_bytes=64)
         w_raw = {}
 
-        def load_w(h, o0, o1, n0, n1):
-            t = keep.tile([P, n1 - n0, (o1 - o0) * I], BF16, name="w_raw_%d_%d_%d" % (h, o0, n0), align_bytes=64)
-            nc.sync.dma_start(out=t[:], in_=Wr[n0:n1, h * P:(h + 1) * P, o0:o1, :].rearrange("n j o i -> j n (o i)"))
-            w_raw[(h, o0, n0)] = t
+        def load_p(t0, t1):
+            nc.sync.dma_start(out=p_raw[:, t0:t1, :], in_=p_rows[:, t0:t1, :])
 
-        if P_FIRST:
-            nc.sync.dma_start(out=p_raw[:, 0:2, :], in_=p2[:, 0:2, :])
-        for n0 in range(0, N, 8):
-            load_w(0, 0, 16, n0, n0 + 8)
-        if not P_FIRST:
-            nc.sync.dma_start(out=p_raw[:, 0:2, :], in_=p2[:, 0:2, :])
-        nc.sync.dma_start(out=p_raw[:, 2:4, :], in_=p2[:, 2:4, :])
-        for n0 in range(0, N, 8):
-            load_w(1, 0, 16, n0, n0 + 8)
-        nc.sync.dma_start(out=p_raw[:, 4:TILES, :], in_=p2[:, 4:TILES, :])
+        def load_w(h):
+            for n0 in range(0, N, N_CHUNK):
+                chunk = keep.tile([P, N_CHUNK, O * I], BF16, name="w_raw_%d_%d" % (h, n0), align_bytes=64)
+                nc.sync.dma_start(
+                    out=chunk[:], in_=Wr[n0:n0 + N_CHUNK, h * P:(h + 1) * P].rearrange("n j o i -> j n (o i)")
+                )
+                w_raw[(h, n0)] = chunk
+
+        load_p(0, 2)
+        load_w(0)
+        load_p(2, 4)
+        load_w(1)
+        load_p(4, TILES)
 
         ident = keep.tile([P, P], F32, name="ident")
         make_identity(nc, ident[:])
 
         w_sorted = [keep.tile([P, O, 2, N, 4], F32, name="w_sorted%d" % h, align_bytes=64) for h in range(HALVES)]
-        w_codes = [[keep.tile([P, 4 * P], U32, name="w_codes%d_%d" % (h, c), align_bytes=64) for c in range(QUADS)] for h in range(HALVES)]
-        w_scales = [[keep.tile([P, 4 * P], U8, name="w_scales%d_%d" % (h, c), align_bytes=64) for c in range(QUADS)] for h in range(HALVES)]
+        w_codes = [
+            [keep.tile([P, BANK], U32, name="w_codes%d_%d" % (h, c), align_bytes=64) for c in range(QUADS)]
+            for h in range(HALVES)
+        ]
+        w_scales = [
+            [keep.tile([P, BANK], U8, name="w_scales%d_%d" % (h, c), align_bytes=64) for c in range(QUADS)]
+            for h in range(HALVES)
+        ]
         p_codes = keep.tile([P, B], U32, name="p_codes", align_bytes=64)
         p_scales = keep.tile([P, B], U8, name="p_scales", align_bytes=64)
-
-        def sort_w(h, n0, o0=0, o1=O):
-            src = w_raw[(h, 0, n0)][:].rearrange("p n x -> p (n x)").bitcast(F32)
-            nc.vector.tensor_copy(
-                out=w_sorted[h][:, o0:o1, :, n0:n0 + 8, :],
-                in_=src.rearrange("p (n o i u) -> p o u n i", n=8, i=4, u=2)[:, o0:o1],
-            )
-
         turned = {}
         grouped = {}
 
-        def turn_w(h, pair, bank_index):
-            t = bank(bank_index, [P, 2, 2, P])
-            for i in range(2):
-                for u in range(2):
-                    nc.tensor.transpose(
-                        t[:, i, u, :], w_sorted[h][:, 2 * pair + i, u, :, :].rearrange("p n i -> p (n i)"), ident[:]
-                    )
-            turned[("w", h, pair)] = t
+        def sort_w(h, n0, o0, o1):
+            words = w_raw[(h, n0)][:].rearrange("p n x -> p (n x)").bitcast(F32)
+            nc.vector.tensor_copy(
+                out=w_sorted[h][:, o0:o1, :, n0:n0 + N_CHUNK, :],
+                in_=words.rearrange("p (n o r u) -> p o u n r", n=N_CHUNK, r=4, u=2)[:, o0:o1],
+            )
 
-        def turn_p(g, bank_index):
-            t = bank(bank_index, [P, 2, 2, P])
-            for i in range(2):
-                words = p_raw[:, 2 * g + i, :].bitcast(F32)
+        def turn(item, bank_index):
+            kind, h, index = item
+            turned[item] = bank(bank_index, [P, 2, 2, P])
+            for x in range(2):
                 for u in range(2):
-                    nc.tensor.transpose(t[:, i, u, :], words[:, u:2 * P:2], ident[:])
-            turned[("p", g)] = t
+                    if kind == "w":
+                        words = w_sorted[h][:, 2 * index + x, u, :, :].rearrange("p n r -> p (n r)")
+                    else:
+                        words = p_raw[:, 2 * index + x, :].bitcast(F32)[:, u:2 * P:2]
+                    nc.tensor.transpose(turned[item][:, x, u, :], words, ident[:])
 
-        def copy_on(engine, dst, src):
-            if engine == "scalar":
-                nc.scalar.copy(out=dst, in_=src)
+        def group(item, copy):
+            kind, h, index = item
+            if kind == "p":
+                grouped[item] = work.tile([P, 2 * BANK], BF16, name="p_grouped", align_bytes=64)
+                dst = grouped[item][:]
             else:
-                nc.vector.tensor_copy(out=dst, in_=src)
+                if index % 2 == 0:
+                    grouped[(kind, h, index // 2)] = work.tile([P, 4 * BANK], BF16, name="w_grouped", align_bytes=64)
+                dst = grouped[(kind, h, index // 2)][:, (index % 2) * 2 * BANK:(index % 2 + 1) * 2 * BANK]
+            copy(
+                out=dst.bitcast(F32).rearrange("p (x c u) -> p x c u", x=2, u=2),
+                in_=turned[item][:].rearrange("p x u c -> p x c u"),
+            )
 
-        def group_w(h, pair, engine):
-            if pair % 2 == 0:
-                grouped[("w", h, pair // 2)] = work.tile([P, 16 * P], BF16, name="w_grouped", align_bytes=64)
-            dst = grouped[("w", h, pair // 2)][:, (pair % 2) * 8 * P:(pair % 2 + 1) * 8 * P].bitcast(F32)
-            copy_on(engine, dst.rearrange("p (o j u) -> p o j u", o=2, u=2), turned[("w", h, pair)][:].rearrange("p o u j -> p o j u"))
+        def quantize(item):
+            kind, h, index = item
+            if kind == "p":
+                cols = slice(2 * P * index, 2 * P * (index + 1))
+                nc.vector.quantize_mx(out=p_codes[:, cols].bitcast(FP8X4), scales=p_scales[:, cols], in_=grouped[item][:])
+            elif index % 2 == 1:
+                c = index // 2
+                nc.vector.quantize_mx(
+                    out=w_codes[h][c][:].bitcast(FP8X4), scales=w_scales[h][c][:], in_=grouped[(kind, h, c)][:]
+                )
 
-        def group_p(g, engine):
-            grouped[("p", g)] = work.tile([P, 8 * P], BF16, name="p_grouped", align_bytes=64)
-            dst = grouped[("p", g)][:].bitcast(F32)
-            copy_on(engine, dst.rearrange("p (t b u) -> p t b u", t=2, u=2), turned[("p", g)][:].rearrange("p t u b -> p t b u"))
-
-        def quantize_w(h, c):
-            nc.vector.quantize_mx(out=w_codes[h][c][:].bitcast(FP8X4), scales=w_scales[h][c][:], in_=grouped[("w", h, c)][:])
-
-        def quantize_p(g):
-            nc.vector.quantize_mx(out=p_codes[:, 2 * g * P:2 * (g + 1) * P].bitcast(FP8X4), scales=p_scales[:, 2 * g * P:2 * (g + 1) * P], in_=grouped[("p", g)][:])
-
-        norm_slots = [(s, k) for s, (h, t0, nb) in enumerate(STEPS) for k in range(QUADS * nb)]
-        out_slots = [(s, t0 + i, c) for s, (h, t0, nb) in enumerate(STEPS) for i in range(nb) for c in range(QUADS)]
-        slots = len(norm_slots)
-        last = len(STEPS) - 1
-        sum_slot = {s: slot + {"D1": DIRECT_LAG, "T2": SUM_LAG, "T1": SINGLE_LAG, "V1": RED_LAG + 3, "D2": DIRECT_LAG}[PLAN.split()[s]] for slot, (s, k) in enumerate(norm_slots)}
         norm_banks = {}
         squares = {}
-        totals = {}
-        parts = {s: [] for s in range(len(STEPS))}
+        pair_sums = {}
         q_of = {}
-        small = {}
-        out_tiles = {}
-        prod_banks = {}
+        roots_of = {}
+        norm_of = {}
+        factor_of = {}
 
-        def p_operand(t0, nb):
-            cols = slice(t0 * P, (t0 + nb) * P)
-            return p_codes[:, cols].bitcast(FP8X4), p_scales[:, cols]
-
-        def by_rows(h, t, c, bank_index):
-            acc = bank(bank_index, [P, 4 * P])
-            codes, scales = p_operand(t, 1)
-            nc.tensor.matmul_mx(out=acc[:], lhsT=codes, lhsT_scale=scales, rhs=w_codes[h][c][:].bitcast(FP8X4),
-                                rhs_scale=w_scales[h][c][:], start=True, stop=True)
-            return acc
-
-        def matmul_for_norm(slot):
-            s, k = norm_slots[slot]
-            h, t0, nb = STEPS[s]
-            per_bank = 4 // nb
-            banks = NORM_BANKS
-            if ROUTE[s] == "V":
-                norm_banks[slot] = by_rows(h, t0, k, banks[slot % len(banks)])
-                return
-            acc = bank(banks[slot % len(banks)], [P, per_bank, nb * P])
-            codes, scales = p_operand(t0, nb)
-            for i in range(per_bank):
-                c, o4 = divmod(k * per_bank + i, 4)
-                cols = slice(o4 * P, (o4 + 1) * P)
-                nc.tensor.matmul_mx(out=acc[:, i, :], lhsT=w_codes[h][c][:, cols].bitcast(FP8X4), lhsT_scale=w_scales[h][c][:, cols],
-                                    rhs=codes, rhs_scale=scales, start=True, stop=True)
-            norm_banks[slot] = acc
+        def norm_product(slot):
+            step, pair = divmod(slot, STEP_SLOTS)
+            h, g = divmod(step, GROUPS)
+            rows = slice(2 * P * g, 2 * P * (g + 1))
+            norm_banks[slot] = bank(NORM_BANKS[slot % len(NORM_BANKS)], [P, 2, 2 * P])
+            for x in range(2):
+                c, o_in_quad = divmod(2 * pair + x, 4)
+                cols = slice(o_in_quad * P, (o_in_quad + 1) * P)
+                nc.tensor.matmul_mx(
+                    out=norm_banks[slot][:, x, :],
+                    lhsT=w_codes[h][c][:, cols].bitcast(FP8X4),
+                    lhsT_scale=w_scales[h][c][:, cols],
+                    rhs=p_codes[:, rows].bitcast(FP8X4),
+                    rhs_scale=p_scales[:, rows],
+                    start=True,
+                    stop=True,
+                )
 
         def square(slot):
-            s, k = norm_slots[slot]
             if slot % 4 == 0:
-                squares[slot // 4] = work.tile([P, 4, 4 * P], F32, name="sq", bufs=4)
-            sq = squares[slot // 4]
-            if ROUTE[s] == "V":
-                dst = sq[:].rearrange("p a x -> p (a x)").rearrange("p (j o) -> p j o", o=O)[:, :, 4 * k:4 * k + 4]
-                nc.scalar.activation(out=dst, in_=norm_banks[slot][:].rearrange("p (o j) -> p j o", o=4), func=ACT.Square, scale=1.0 / K)
-                return
-            nc.scalar.activation(out=sq[:, slot % 4, :], in_=norm_banks[slot][:].rearrange("p o b -> p (o b)"), func=ACT.Square, scale=1.0 / K)
-            if ROUTE[s] == "D":
-                parts[s].append(sq[:, slot % 4, :])
+                squares[slot // 4] = work.tile([P, 4, BANK], F32, name="squares", bufs=5)
+            nc.scalar.activation(
+                out=squares[slot // 4][:, slot % 4, :],
+                in_=norm_banks[slot][:].rearrange("p x b -> p (x b)"),
+                func=ACT.Square,
+                scale=1.0 / K,
+            )
 
-        def add_pair(slot, count):
-            sq = squares[slot // 4]
-            if slot % 4 == 2 * count - 1:
-                totals[slot // 4] = work.tile([P, 2, 4 * P], F32, name="pair_sum", bufs=4)
-            total = totals[slot // 4]
-            engine = nc.vector if slot < V_ADDS else nc.gpsimd
-            if count == 2:
-                engine.tensor_tensor(out=total[:], in0=sq[:, 0:2, :], in1=sq[:, 2:4, :], op=ALU.add)
-                parts[norm_slots[slot][0]].extend([total[:, 0, :], total[:, 1, :]])
-            else:
-                a = (slot % 4) // 2
-                engine.tensor_tensor(out=total[:, a, :], in0=sq[:, 2 * a, :], in1=sq[:, 2 * a + 1, :], op=ALU.add)
-                parts[norm_slots[slot][0]].append(total[:, a, :])
-
-        def sum_squares(s, half, halves):
-            nb = STEPS[s][2]
+        def add_pair(slot, engine):
+            half = slot % 4 // 2
             if half == 0:
-                q_of[s] = bank(Q_BANK if s != last else TAILQ, [P, nb, P])
-            count = (4 if ROUTE[s] == "D" else 2) * nb
-            for i in range(half * count // halves, (half + 1) * count // halves):
-                for x in range(4):
-                    nc.tensor.matmul(out=q_of[s][:, x % nb, :], lhsT=parts[s][i][:, x * P:(x + 1) * P], rhs=ident[:], is_transpose=True,
-                                     start=(i == 0 and x == 0), stop=(i == count - 1 and x == 3))
+                pair_sums[slot // 4] = work.tile([P, 2, BANK], F32, name="pair_sums", bufs=4)
+            sq = squares[slot // 4]
+            engine.tensor_tensor(
+                out=pair_sums[slot // 4][:, half, :], in0=sq[:, 2 * half, :], in1=sq[:, 2 * half + 1, :], op=ALU.add
+            )
 
-        def reduce_squares(s, first_slot, quarter):
-            if quarter == 0:
-                q_of[s] = work.tile([P, 1, P], F32, name="q_sbuf")
-            nc.vector.tensor_reduce(out=q_of[s][:, 0, quarter * 32:(quarter + 1) * 32], in_=squares[first_slot // 4][:, quarter, :].rearrange("p (j o) -> p j o", o=O),
-                                    axis=mybir.AxisListType.X, op=ALU.add)
+        def sum_squares(step):
+            q_of[step] = bank(Q_BANK if step < STEPS - 1 else NORM_BANKS[0], [P, 2, P])
+            blocks = [
+                (x % 2, pair_sums[2 * step + a][:, half, x * P:(x + 1) * P])
+                for a in range(2) for half in range(2) for x in range(4)
+            ]
+            for n, (tile, block) in enumerate(blocks):
+                nc.tensor.matmul(
+                    out=q_of[step][:, tile, :], lhsT=block, rhs=ident[:], is_transpose=True,
+                    start=(n == 0), stop=(n == len(blocks) - 1),
+                )
 
-        def roots(s):
-            nb = STEPS[s][2]
-            a = work.tile([P, nb, P], F32, name="inv_norm")
-            g = work.tile([P, nb, P], F32, name="inv_root")
-            u = work.tile([P, nb, P], F32, name="inv_one_plus")
-            nc.scalar.activation(out=g[:], in_=q_of[s][:], func=ACT.Abs_reciprocal_sqrt, scale=1.0, bias=1.0)
-            nc.scalar.activation(out=a[:], in_=q_of[s][:], func=ACT.Abs_reciprocal_sqrt, scale=float(K * K), bias=K * K * SQ_EPS)
-            if U_ON_G and ROUTE[s] != "D" and s > 0:
-                nc.gpsimd.tensor_tensor(out=u[:], in0=g[:], in1=g[:], op=ALU.mult)
-            else:
-                nc.scalar.activation(out=u[:], in_=g[:], func=ACT.Square)
-            small[s] = (a, u)
+        def roots(step):
+            inv_norm = work.tile([P, 2, P], F32, name="inv_norm")
+            inv_root = work.tile([P, 2, P], F32, name="inv_root")
+            inv_one_plus = work.tile([P, 2, P], F32, name="inv_one_plus")
+            q = q_of[step][:]
+            nc.scalar.activation(out=inv_root[:], in_=q, func=ACT.Abs_reciprocal_sqrt, scale=1.0, bias=1.0)
+            nc.scalar.activation(
+                out=inv_norm[:], in_=q, func=ACT.Abs_reciprocal_sqrt, scale=float(K * K), bias=K * K * SQ_EPS
+            )
+            nc.scalar.activation(out=inv_one_plus[:], in_=inv_root[:], func=ACT.Square)
+            roots_of[step] = (inv_norm, inv_one_plus)
 
-        def norm_times(s):
-            t = work.tile([P, STEPS[s][2], P], F32, name="norm")
-            engine = nc.gpsimd if ROUTE[s] == "V" else nc.vector
-            engine.tensor_tensor(out=t[:], in0=q_of[s][:], in1=small[s][0][:], op=ALU.mult)
-            small[s] = (t, small[s][1])
+        def norm_times(step):
+            norm_of[step] = work.tile([P, 2, P], F32, name="norm")
+            nc.vector.tensor_tensor(out=norm_of[step][:], in0=q_of[step][:], in1=roots_of[step][0][:], op=ALU.mult)
 
-        def factor(s):
-            f = work.tile([P, STEPS[s][2], P], F32, name="factor", bufs=4)
-            engine = nc.vector if s == 0 or (s == last and G_TILE < 0) else nc.gpsimd
-            engine.tensor_tensor(out=f[:], in0=small[s][0][:], in1=small[s][1][:], op=ALU.mult)
-            small[s] = f
+        def factor(step):
+            factor_of[step] = work.tile([P, 2, P], F32, name="factor", bufs=4)
+            engine = nc.vector if step in (0, STEPS - 1) else nc.gpsimd
+            engine.tensor_tensor(out=factor_of[step][:], in0=norm_of[step][:], in1=roots_of[step][1][:], op=ALU.mult)
 
-        def matmul_for_out(m, bank_index):
-            s, t, c = out_slots[m]
-            prod_banks[m] = by_rows(STEPS[s][0], t, c, bank_index)
+        out_banks = {}
+        out_tiles = {}
 
-        def copy_out(m):
-            s, t, c = out_slots[m]
-            h = STEPS[s][0]
-            if c == 0:
-                out_tiles[(h, t)] = work.tile([P, P, O], F32, name="plain_tile", bufs=1)
-            nc.scalar.copy(out=out_tiles[(h, t)][:, :, 4 * c:4 * c + 4], in_=prod_banks[m][:].rearrange("p (o j) -> p j o", o=4))
-
-        def scale_on_gpsimd(m, j0, j1):
-            s, t, c = out_slots[m]
-            h, t0, nb = STEPS[s]
-            part = out_tiles[(h, t)][:, j0:j1, :]
-            nc.gpsimd.tensor_tensor(out=part, in0=part, in1=small[s][:, t - t0, j0:j1].unsqueeze(2).to_broadcast([P, j1 - j0, O]), op=ALU.mult)
-
-        def store_part(m, j0, j1):
-            s, t, c = out_slots[m]
-            h = STEPS[s][0]
-            nc.sync.dma_start(out=out2[t * P:(t + 1) * P, (h * P + j0) * O:(h * P + j1) * O],
-                              in_=out_tiles[(h, t)][:, j0:j1, :].rearrange("p j o -> p (j o)"))
+        def out_product(m, bank_index):
+            h, t, c = m // (TILES * QUADS), m // QUADS % TILES, m % QUADS
+            rows = slice(P * t, P * (t + 1))
+            out_banks[m] = bank(bank_index, [P, BANK])
+            nc.tensor.matmul_mx(
+                out=out_banks[m][:],
+                lhsT=p_codes[:, rows].bitcast(FP8X4),
+                lhsT_scale=p_scales[:, rows],
+                rhs=w_codes[h][c][:].bitcast(FP8X4),
+                rhs_scale=w_scales[h][c][:],
+                start=True,
+                stop=True,
+            )
 
         def scale_out(m, j0, j1):
-            s, t, c = out_slots[m]
-            h, t0, nb = STEPS[s]
+            h, t, c = m // (TILES * QUADS), m // QUADS % TILES, m % QUADS
             if c == 0 and j0 == 0:
-                out_tiles[(h, t)] = work.tile([P, P, O], F32, name="out_tile", bufs=4)
+                out_tiles[m // QUADS] = work.tile([P, P, O], F32, name="out_tile", bufs=4)
+            result = out_tiles[m // QUADS]
             nc.vector.tensor_tensor(
-                out=out_tiles[(h, t)][:, j0:j1, 4 * c:4 * c + 4],
-                in0=prod_banks[m][:].rearrange("p (o j) -> p j o", o=4)[:, j0:j1, :],
-                in1=small[s][:, t - t0, j0:j1].unsqueeze(2).to_broadcast([P, j1 - j0, 4]),
+                out=result[:, j0:j1, 4 * c:4 * c + 4],
+                in0=out_banks[m][:].rearrange("p (o j) -> p j o", o=4)[:, j0:j1, :],
+                in1=factor_of[m // STEP_SLOTS][:, t % 2, j0:j1].unsqueeze(2).to_broadcast([P, j1 - j0, 4]),
                 op=ALU.mult,
             )
             if c == QUADS - 1:
-                nc.sync.dma_start(out=out2[t * P:(t + 1) * P, (h * P + j0) * O:(h * P + j1) * O],
-                                  in_=out_tiles[(h, t)][:, j0:j1, :].rearrange("p j o -> p (j o)"))
+                nc.sync.dma_start(
+                    out=out_rows[P * t:P * (t + 1), (h * P + j0) * O:(h * P + j1) * O],
+                    in_=result[:, j0:j1, :].rearrange("p j o -> p (j o)"),
+                )
 
-        engine_of = {"s": "scalar", "v": "vector"}
-        if WARM:
-            zeros = keep.tile([P, 4 * P], BF16, name="zeros")
-            nc.vector.memset(zeros[:], 0.0)
-            scratch = bank(0, [P, 4 * P])
-            for n in range(WARM):
-                nc.tensor.matmul(out=scratch[:], lhsT=zeros[:, 0:P], rhs=zeros[:], start=True, stop=True)
-
-        if P_FIRST:
-            turn_p(0, 0)
-            group_p(0, "scalar")
-        sort_w(0, 0)
-        if P_FIRST:
-            quantize_p(0)
-        sort_w(0, 8)
-        sort_w(0, 16)
-        sort_w(0, 24, 0, 8)
-        sort_w(0, 24, 8, 16)
-        for pair in range(8):
-            turn_w(0, pair, [3, 4, 5, 6, 7, 1, 2][pair % 7])
-            if pair == 3 and not P_FIRST:
-                turn_p(0, 0)
-            group_w(0, pair, engine_of[HEAD_ENG[pair]])
-            if pair == 3 and not P_FIRST:
-                group_p(0, "vector")
-            if pair == 4 and not P_FIRST:
-                quantize_p(0)
+        first_group = ("p", 0, 0)
+        turn(first_group, NORM_BANKS[0])
+        group(first_group, nc.scalar.copy)
+        sort_w(0, 0, 0, O)
+        quantize(first_group)
+        for n0 in range(N_CHUNK, N - N_CHUNK, N_CHUNK):
+            sort_w(0, n0, 0, O)
+        sort_w(0, N - N_CHUNK, 0, O // 2)
+        sort_w(0, N - N_CHUNK, O // 2, O)
+        head_banks = OUT_BANKS + (NORM_BANKS[3], Q_BANK, NORM_BANKS[1], NORM_BANKS[2])
+        for pair in range(PAIRS):
+            item = ("w", 0, pair)
+            turn(item, head_banks[pair % len(head_banks)])
+            group(item, nc.vector.tensor_copy if pair == 1 else nc.scalar.copy)
             if pair % 2 == 1:
-                quantize_w(0, pair // 2)
-            for n in range(4):
-                if SORT_AT[n] == pair:
-                    sort_w(1, 8 * n)
-        for n in range(4):
-            if SORT_AT[n] == 8:
-                sort_w(1, 8 * n)
+                quantize(item)
+                sort_w(1, N_CHUNK * (pair // 2), 0, O)
 
-        prep = [("p", 1), ("w", 0), ("w", 1), ("w", 2), ("w", 3), ("p", 2), ("w", 4), ("w", 5), ("p", 3), ("w", 6), ("w", 7)]
-        events = []
+        later = [("w", 1, pair) for pair in range(PAIRS)]
+        later = later[:2] + [("p", 0, 2)] + later[2:4] + [("p", 0, 3)] + later[4:]
+        prep = [(1, ("p", 0, 1))]
+        prep += [(PREP_START + PREP_EVERY * (n // len(OUT_BANKS)), item) for n, item in enumerate(later)]
 
-        def at(key, call, *args):
-            events.append((key, len(events), call, args))
+        out_delay = STEP_SLOTS - 1 + OUT_LAG
+        for slot in range(SLOTS + out_delay - QUADS):
+            m = slot - out_delay
+            step, since_sum = divmod(slot - (STEP_SLOTS - 1 + SUM_LAG), STEP_SLOTS)
+            summing = 0 <= step < STEPS
+            if m >= 0:
+                out_product(m, OUT_BANKS[m % len(OUT_BANKS)])
+            if slot < SLOTS:
+                norm_product(slot)
+            if summing and since_sum == 1:
+                roots(step)
+            if summing and since_sum == 2:
+                norm_times(step)
+            if slot < SLOTS:
+                square(slot)
+            if summing and since_sum == 2:
+                factor(step)
+            if slot % 2 == 1 and VECTOR_ADD_STEPS * STEP_SLOTS <= slot < SLOTS:
+                add_pair(slot, nc.gpsimd)
+            if slot % 2 == 0 and 0 < slot <= VECTOR_ADD_STEPS * STEP_SLOTS:
+                add_pair(slot - 1, nc.vector)
+            if m >= 0:
+                scale_out(m, 0, P)
+            if summing and since_sum == 0:
+                sum_squares(step)
+            for n, (place, item) in enumerate(prep):
+                if place == slot:
+                    turn(item, OUT_BANKS[n % len(OUT_BANKS)])
+            for n, (place, item) in enumerate(prep):
+                if place == slot:
+                    group(item, nc.vector.tensor_copy if n % 2 == 0 else nc.scalar.copy)
+            for place, item in prep:
+                if place + 1 == slot:
+                    quantize(item)
 
-        for slot in range(slots):
-            s, k = norm_slots[slot]
-            at(slot, matmul_for_norm, slot)
-            at(slot + 0.5, square, slot)
-            count = 1 if slot < V_ADDS else GB
-            if ROUTE[s] == "T" and slot % (2 * count) == 2 * count - 1:
-                at(slot + (V_ADD_LAG if slot < V_ADDS else 0.55), add_pair, slot, count)
-            if ROUTE[s] == "V" and k == 3:
-                for quarter in range(4):
-                    at(slot + RED_LAG + quarter + 0.75, reduce_squares, s, slot - 3, quarter)
-        for s in range(len(STEPS)):
-            halves = 2 if STEPS[s][2] == 2 or s == last else 1
-            if ROUTE[s] != "V":
-                for half in range(halves):
-                    at(sum_slot[s] - (halves - 1 - half) * QUADS * STEPS[s][2] // halves + 0.8, sum_squares, s, half, halves)
-            at(sum_slot[s] + ROOT_LAG + 0.3, roots, s)
-            at(sum_slot[s] + NORM_LAG + 0.3, norm_times, s)
-            at(sum_slot[s] + FAC_LAG + FAC_KEY, factor, s)
-        slot = FIRST_OUT
-        todo = [m for m in range(len(out_slots) - QUADS) if m // QUADS != G_TILE]
-        n = 0
-        while n < len(todo):
-            for extra in range(2 if slot % CATCH_UP == 0 else 1):
-                if n < len(todo) and slot >= sum_slot[out_slots[todo[n]][0]] + OUT_LAG:
-                    at(slot + B_KEY, matmul_for_out, todo[n], OUT_BANKS[n % len(OUT_BANKS)])
-                    at(slot + 0.7, scale_out, todo[n], 0, P)
-                    n += 1
-            slot += 1
-        if G_TILE >= 0:
-            for c in range(QUADS):
-                at(slots + c, matmul_for_out, QUADS * G_TILE + c, NORM_BANKS[(slots + c + 1) % 4] if c < 3 else 1)
-                at(slots + c + 0.5, copy_out, QUADS * G_TILE + c)
-            for half in range(2):
-                at(G_KEY + 3 + 0.01 * half, scale_on_gpsimd, QUADS * G_TILE, half * 64, half * 64 + 64)
-                at(G_KEY + 6 + 4 * half, store_part, QUADS * G_TILE, half * 64, half * 64 + 64)
-
-        def turn(kind, index, bank_index):
-            if kind == "p":
-                turn_p(index, bank_index)
-            else:
-                turn_w(1, index, bank_index)
-
-        def group(kind, index, engine):
-            if kind == "p":
-                group_p(index, engine)
-            else:
-                group_w(1, index, engine)
-
-        def quantize(kind, index):
-            if kind == "p":
-                quantize_p(index)
-            elif index % 2 == 1:
-                quantize_w(1, index // 2)
-
-        for n, (kind, index) in enumerate(prep):
-            place = PREP_START + PREP_EVERY * (n // RUN)
-            at(place + 0.85, turn, kind, index, PREP_BANKS[n % RUN])
-            at(place + 0.9, group, kind, index, engine_of[PREP_ENG[n % RUN]])
-            at(place + 0.95, quantize, kind, index)
-        for key, order, call, args in sorted(events, key=lambda e: e[:2]):
-            call(*args)
-        for m in range(len(out_slots) - QUADS, len(out_slots)):
-            matmul_for_out(m, [7, 1, 2, 6][m % 4])
-        for j0 in range(0, P, P // TAIL_SPLIT):
-            for m in range(len(out_slots) - QUADS, len(out_slots)):
-                scale_out(m, j0, j0 + P // TAIL_SPLIT)
+        tail_banks = (Q_BANK,) + NORM_BANKS[1:]
+        last_tile = range(SLOTS - QUADS, SLOTS)
+        for m in last_tile:
+            out_product(m, tail_banks[m % QUADS])
+        for j0 in (0, P // 2):
+            for m in last_tile:
+                scale_out(m, j0, j0 + P // 2)

@@ -34,6 +34,8 @@ PREP_START = 4
 PREP_EVERY = 3
 VECTOR_ADD_STEPS = 2
 
+WARM_UP = 6
+
 NORM_BANKS = (0, 1, 2, 6)
 OUT_BANKS = (3, 4, 5)
 Q_BANK = 7
@@ -75,6 +77,9 @@ def tile_capsulenetwork_pb_kernel(tc, p, Wr, out):
 
         ident = keep.tile([P, P], F32, name="ident")
         make_identity(nc, ident[:])
+
+        unread_column = keep.tile([P, 1], F32, name="unread_column")
+        nc.scalar.activation(out=unread_column[:], in_=ident[:, 0:1], func=ACT.Abs_reciprocal_sqrt, scale=1.0, bias=1.0)
 
         w_sorted = [keep.tile([P, O, 2, N, 4], F32, name="w_sorted%d" % h, align_bytes=64) for h in range(HALVES)]
         w_codes = [
@@ -254,6 +259,10 @@ def tile_capsulenetwork_pb_kernel(tc, p, Wr, out):
             sort_w(0, n0, 0, O)
         sort_w(0, N - N_CHUNK, 0, O // 2)
         sort_w(0, N - N_CHUNK, O // 2, O)
+        early = w_raw[(0, N_CHUNK)][:].rearrange("p n x -> p (n x)")
+        unread = bank(NORM_BANKS[1], [P, BANK])
+        for n in range(WARM_UP):
+            nc.tensor.matmul(out=unread[:], lhsT=early[:, 0:P], rhs=early[:, 0:BANK], start=True, stop=True)
         head_banks = OUT_BANKS + (NORM_BANKS[3], Q_BANK, NORM_BANKS[1], NORM_BANKS[2])
         for pair in range(PAIRS):
             item = ("w", 0, pair)

from contextlib import ExitStack

import concourse.mybir as mybir
from concourse.masks import make_identity

B, N, I, K, O = 1024, 32, 16, 256, 16
FLOPS = 2 * B * N * I * K * O
SQ_EPS = 1e-8

F32 = mybir.dt.float32
BF16 = mybir.dt.bfloat16
U32 = mybir.dt.uint32
U8 = mybir.dt.uint8
FP8X4 = mybir.dt.float8_e5m2_x4
ACT = mybir.ActivationFunctionType
ALU = mybir.AluOpType

P = 128
BANK = 512
HALVES = K // P
TILES = B // P
GROUPS = TILES // 2
QUADS = O // 4
PAIRS = O // 2
N_CHUNK = 8

STEPS = HALVES * GROUPS
STEP_SLOTS = PAIRS
SLOTS = STEPS * STEP_SLOTS

SUM_LAG = 4
OUT_LAG = 10
PREP_START = 4
PREP_EVERY = 3
VECTOR_ADD_STEPS = 2

WARM_UP = 6

NORM_BANKS = (0, 1, 2, 6)
OUT_BANKS = (3, 4, 5)
Q_BANK = 7


def tile_capsulenetwork_pb_kernel(tc, p, Wr, out):
    nc = tc.nc
    p_rows = p.rearrange("(t b) n i -> b t (n i)", b=P)
    out_rows = out.rearrange("b j o -> b (j o)")

    with ExitStack() as ctx:
        keep = ctx.enter_context(tc.tile_pool(name="keep", bufs=1))
        work = ctx.enter_context(tc.tile_pool(name="work", bufs=3))
        psum = ctx.enter_context(tc.psum_pool(name="psum", bufs=1))
        ctx.enter_context(tc.manual_schedule())

        def bank(index, shape):
            return psum.tile(shape, F32, name="bank%d" % index, tag="bank%d" % index)

        p_raw = keep.tile([P, TILES, N * I], BF16, name="p_raw", align_bytes=64)
        w_raw = {}

        def load_p(t0, t1):
            nc.sync.dma_start(out=p_raw[:, t0:t1, :], in_=p_rows[:, t0:t1, :])

        def load_w(h):
            for n0 in range(0, N, N_CHUNK):
                chunk = keep.tile([P, N_CHUNK, O * I], BF16, name="w_raw_%d_%d" % (h, n0), align_bytes=64)
                nc.sync.dma_start(
                    out=chunk[:], in_=Wr[n0:n0 + N_CHUNK, h * P:(h + 1) * P].rearrange("n j o i -> j n (o i)")
                )
                w_raw[(h, n0)] = chunk

        load_p(0, 2)
        load_w(0)
        load_p(2, 4)
        load_w(1)
        load_p(4, TILES)

        ident = keep.tile([P, P], F32, name="ident")
        make_identity(nc, ident[:])

        unread_column = keep.tile([P, 1], F32, name="unread_column")
        nc.scalar.activation(out=unread_column[:], in_=ident[:, 0:1], func=ACT.Abs_reciprocal_sqrt, scale=1.0, bias=1.0)

        w_sorted = [keep.tile([P, O, 2, N, 4], F32, name="w_sorted%d" % h, align_bytes=64) for h in range(HALVES)]
        w_codes = [
            [keep.tile([P, BANK], U32, name="w_codes%d_%d" % (h, c), align_bytes=64) for c in range(QUADS)]
            for h in range(HALVES)
        ]
        w_scales = [
            [keep.tile([P, BANK], U8, name="w_scales%d_%d" % (h, c), align_bytes=64) for c in range(QUADS)]
            for h in range(HALVES)
        ]
        p_codes = keep.tile([P, B], U32, name="p_codes", align_bytes=64)
        p_scales = keep.tile([P, B], U8, name="p_scales", align_bytes=64)
        turned = {}
        grouped = {}

        def sort_w(h, n0, o0, o1):
            words = w_raw[(h, n0)][:].rearrange("p n x -> p (n x)").bitcast(F32)
            nc.vector.tensor_copy(
                out=w_sorted[h][:, o0:o1, :, n0:n0 + N_CHUNK, :],
                in_=words.rearrange("p (n o r u) -> p o u n r", n=N_CHUNK, r=4, u=2)[:, o0:o1],
            )

        def turn(item, bank_index):
            kind, h, index = item
            turned[item] = bank(bank_index, [P, 2, 2, P])
            for x in range(2):
                for u in range(2):
                    if kind == "w":
                        words = w_sorted[h][:, 2 * index + x, u, :, :].rearrange("p n r -> p (n r)")
                    else:
                        words = p_raw[:, 2 * index + x, :].bitcast(F32)[:, u:2 * P:2]
                    nc.tensor.transpose(turned[item][:, x, u, :], words, ident[:])

        def group(item, copy):
            kind, h, index = item
            if kind == "p":
                grouped[item] = work.tile([P, 2 * BANK], BF16, name="p_grouped", align_bytes=64)
                dst = grouped[item][:]
            else:
                if index % 2 == 0:
                    grouped[(kind, h, index // 2)] = work.tile([P, 4 * BANK], BF16, name="w_grouped", align_bytes=64)
                dst = grouped[(kind, h, index // 2)][:, (index % 2) * 2 * BANK:(index % 2 + 1) * 2 * BANK]
            copy(
                out=dst.bitcast(F32).rearrange("p (x c u) -> p x c u", x=2, u=2),
                in_=turned[item][:].rearrange("p x u c -> p x c u"),
            )

        def quantize(item):
            kind, h, index = item
            if kind == "p":
                cols = slice(2 * P * index, 2 * P * (index + 1))
                nc.vector.quantize_mx(out=p_codes[:, cols].bitcast(FP8X4), scales=p_scales[:, cols], in_=grouped[item][:])
            elif index % 2 == 1:
                c = index // 2
                nc.vector.quantize_mx(
                    out=w_codes[h][c][:].bitcast(FP8X4), scales=w_scales[h][c][:], in_=grouped[(kind, h, c)][:]
                )

        norm_banks = {}
        squares = {}
        pair_sums = {}
        q_of = {}
        roots_of = {}
        norm_of = {}
        factor_of = {}

        def norm_product(slot):
            step, pair = divmod(slot, STEP_SLOTS)
            h, g = divmod(step, GROUPS)
            rows = slice(2 * P * g, 2 * P * (g + 1))
            norm_banks[slot] = bank(NORM_BANKS[slot % len(NORM_BANKS)], [P, 2, 2 * P])
            for x in range(2):
                c, o_in_quad = divmod(2 * pair + x, 4)
                cols = slice(o_in_quad * P, (o_in_quad + 1) * P)
                nc.tensor.matmul_mx(
                    out=norm_banks[slot][:, x, :],
                    lhsT=w_codes[h][c][:, cols].bitcast(FP8X4),
                    lhsT_scale=w_scales[h][c][:, cols],
                    rhs=p_codes[:, rows].bitcast(FP8X4),
                    rhs_scale=p_scales[:, rows],
                    start=True,
                    stop=True,
                )

        def square(slot):
            if slot % 4 == 0:
                squares[slot // 4] = work.tile([P, 4, BANK], F32, name="squares", bufs=5)
            nc.scalar.activation(
                out=squares[slot // 4][:, slot % 4, :],
                in_=norm_banks[slot][:].rearrange("p x b -> p (x b)"),
                func=ACT.Square,
                scale=1.0 / K,
            )

        def add_pair(slot, engine):
            half = slot % 4 // 2
            if half == 0:
                pair_sums[slot // 4] = work.tile([P, 2, BANK], F32, name="pair_sums", bufs=4)
            sq = squares[slot // 4]
            engine.tensor_tensor(
                out=pair_sums[slot // 4][:, half, :], in0=sq[:, 2 * half, :], in1=sq[:, 2 * half + 1, :], op=ALU.add
            )

        def sum_squares(step):
            q_of[step] = bank(Q_BANK if step < STEPS - 1 else NORM_BANKS[0], [P, 2, P])
            blocks = [
                (x % 2, pair_sums[2 * step + a][:, half, x * P:(x + 1) * P])
                for a in range(2) for half in range(2) for x in range(4)
            ]
            for n, (tile, block) in enumerate(blocks):
                nc.tensor.matmul(
                    out=q_of[step][:, tile, :], lhsT=block, rhs=ident[:], is_transpose=True,
                    start=(n == 0), stop=(n == len(blocks) - 1),
                )

        def roots(step):
            inv_norm = work.tile([P, 2, P], F32, name="inv_norm")
            inv_root = work.tile([P, 2, P], F32, name="inv_root")
            inv_one_plus = work.tile([P, 2, P], F32, name="inv_one_plus")
            q = q_of[step][:]
            nc.scalar.activation(out=inv_root[:], in_=q, func=ACT.Abs_reciprocal_sqrt, scale=1.0, bias=1.0)
            nc.scalar.activation(
                out=inv_norm[:], in_=q, func=ACT.Abs_reciprocal_sqrt, scale=float(K * K), bias=K * K * SQ_EPS
            )
            nc.scalar.activation(out=inv_one_plus[:], in_=inv_root[:], func=ACT.Square)
            roots_of[step] = (inv_norm, inv_one_plus)

        def norm_times(step):
            norm_of[step] = work.tile([P, 2, P], F32, name="norm")
            nc.vector.tensor_tensor(out=norm_of[step][:], in0=q_of[step][:], in1=roots_of[step][0][:], op=ALU.mult)

        def factor(step):
            factor_of[step] = work.tile([P, 2, P], F32, name="factor", bufs=4)
            engine = nc.vector if step in (0, STEPS - 1) else nc.gpsimd
            engine.tensor_tensor(out=factor_of[step][:], in0=norm_of[step][:], in1=roots_of[step][1][:], op=ALU.mult)

        out_banks = {}
        out_tiles = {}

        def out_product(m, bank_index):
            h, t, c = m // (TILES * QUADS), m // QUADS % TILES, m % QUADS
            rows = slice(P * t, P * (t + 1))
            out_banks[m] = bank(bank_index, [P, BANK])
            nc.tensor.matmul_mx(
                out=out_banks[m][:],
                lhsT=p_codes[:, rows].bitcast(FP8X4),
                lhsT_scale=p_scales[:, rows],
                rhs=w_codes[h][c][:].bitcast(FP8X4),
                rhs_scale=w_scales[h][c][:],
                start=True,
                stop=True,
            )

        def scale_out(m, j0, j1):
            h, t, c = m // (TILES * QUADS), m // QUADS % TILES, m % QUADS
            if c == 0 and j0 == 0:
                out_tiles[m // QUADS] = work.tile([P, P, O], F32, name="out_tile", bufs=4)
            result = out_tiles[m // QUADS]
            nc.vector.tensor_tensor(
                out=result[:, j0:j1, 4 * c:4 * c + 4],
                in0=out_banks[m][:].rearrange("p (o j) -> p j o", o=4)[:, j0:j1, :],
                in1=factor_of[m // STEP_SLOTS][:, t % 2, j0:j1].unsqueeze(2).to_broadcast([P, j1 - j0, 4]),
                op=ALU.mult,
            )
            if c == QUADS - 1:
                nc.sync.dma_start(
                    out=out_rows[P * t:P * (t + 1), (h * P + j0) * O:(h * P + j1) * O],
                    in_=result[:, j0:j1, :].rearrange("p j o -> p (j o)"),
                )

        first_group = ("p", 0, 0)
        turn(first_group, NORM_BANKS[0])
        group(first_group, nc.scalar.copy)
        sort_w(0, 0, 0, O)
        quantize(first_group)
        for n0 in range(N_CHUNK, N - N_CHUNK, N_CHUNK):
            sort_w(0, n0, 0, O)
        sort_w(0, N - N_CHUNK, 0, O // 2)
        sort_w(0, N - N_CHUNK, O // 2, O)
        early = w_raw[(0, N_CHUNK)][:].rearrange("p n x -> p (n x)")
        unread = bank(NORM_BANKS[1], [P, BANK])
        for n in range(WARM_UP):
            nc.tensor.matmul(out=unread[:], lhsT=early[:, 0:P], rhs=early[:, 0:BANK], start=True, stop=True)
        head_banks = OUT_BANKS + (NORM_BANKS[3], Q_BANK, NORM_BANKS[1], NORM_BANKS[2])
        for pair in range(PAIRS):
            item = ("w", 0, pair)
            turn(item, head_banks[pair % len(head_banks)])
            group(item, nc.vector.tensor_copy if pair == 1 else nc.scalar.copy)
            if pair % 2 == 1:
                quantize(item)
                sort_w(1, N_CHUNK * (pair // 2), 0, O)

        later = [("w", 1, pair) for pair in range(PAIRS)]
        later = later[:2] + [("p", 0, 2)] + later[2:4] + [("p", 0, 3)] + later[4:]
        prep = [(1, ("p", 0, 1))]
        prep += [(PREP_START + PREP_EVERY * (n // len(OUT_BANKS)), item) for n, item in enumerate(later)]

        out_delay = STEP_SLOTS - 1 + OUT_LAG
        for slot in range(SLOTS + out_delay - QUADS):
            m = slot - out_delay
            step, since_sum = divmod(slot - (STEP_SLOTS - 1 + SUM_LAG), STEP_SLOTS)
            summing = 0 <= step < STEPS
            if m >= 0:
                out_product(m, OUT_BANKS[m % len(OUT_BANKS)])
            if slot < SLOTS:
                norm_product(slot)
            if summing and since_sum == 1:
                roots(step)
            if summing and since_sum == 2:
                norm_times(step)
            if slot < SLOTS:
                square(slot)
            if summing and since_sum == 2:
                factor(step)
            if slot % 2 == 1 and VECTOR_ADD_STEPS * STEP_SLOTS <= slot < SLOTS:
                add_pair(slot, nc.gpsimd)
            if slot % 2 == 0 and 0 < slot <= VECTOR_ADD_STEPS * STEP_SLOTS:
                add_pair(slot - 1, nc.vector)
            if m >= 0:
                scale_out(m, 0, P)
            if summing and since_sum == 0:
                sum_squares(step)
            for n, (place, item) in enumerate(prep):
                if place == slot:
                    turn(item, OUT_BANKS[n % len(OUT_BANKS)])
            for n, (place, item) in enumerate(prep):
                if place == slot:
                    group(item, nc.vector.tensor_copy if n % 2 == 0 else nc.scalar.copy)
            for place, item in prep:
                if place + 1 == slot:
                    quantize(item)

        tail_banks = (Q_BANK,) + NORM_BANKS[1:]
        last_tile = range(SLOTS - QUADS, SLOTS)
        for m in last_tile:
            out_product(m, tail_banks[m % QUADS])
        for j0 in (0, P // 2):
            for m in last_tile:
                scale_out(m, j0, j0 + P // 2)
